import numpy as np
import ml_dtypes


def mxq(x, axis, fmt="e4m3"):
    dtype, down = {"e4m3": (ml_dtypes.float8_e4m3fn, 7), "e5m2": (ml_dtypes.float8_e5m2, 14)}[fmt]
    v = np.moveaxis(np.asarray(x, np.float32).astype(ml_dtypes.bfloat16).astype(np.float64), axis, -1)
    blocks = v.reshape(v.shape[:-1] + (-1, 32))
    amax = np.abs(blocks).max(-1, keepdims=True)
    byte = np.maximum(np.where(amax > 0, np.frexp(amax)[1] - 1 + 127, 0) - down, 1)
    scale = np.exp2(byte - 127.0)
    codes = (blocks / scale).astype(np.float32).astype(dtype).astype(np.float64)
    return np.moveaxis((codes * scale).reshape(v.shape), -1, axis)


WIDE = False


def mx_kscale(k):
    if not WIDE:
        return np.ones(k)
    levels = np.array([10, -10, 5, -5, 0])
    a = np.random.permutation(np.resize(levels, k // 512 * 4)).reshape(k // 512, 4)
    idx = np.arange(k)
    return np.exp2(a[idx // 512, idx % 128 // 32])


BF16 = ml_dtypes.bfloat16


def bf(x):
    return np.asarray(x, np.float32).astype(BF16)


def f64(x):
    return np.asarray(x).astype(np.float64)


E2M1 = np.array([0.0, 0.5, 1.0, 1.5, 2.0, 3.0, 4.0, 6.0, -0.0, -0.5, -1.0, -1.5, -2.0, -3.0, -4.0, -6.0])


def pack_weight(w, fmt):
    k, n = w.shape
    w = f64(bf(w)).reshape(k // 32, 32, n)
    amax = np.abs(w).max(1)
    if fmt == "e4m3":
        byte = np.frexp(amax)[1] - 1 + 127 - 7
    else:
        mant, ex = np.frexp(amax / 6.0)
        byte = np.where(mant > 0.5, ex, ex - 1) + 127
    byte = np.clip(np.where(amax > 0, byte, 1), 1, 254)
    scaled = (w * np.exp2(127.0 - byte)[:, None, :]).reshape(k, n).astype(np.float32)
    by_word = np.ascontiguousarray(scaled.reshape(k // 512, 128, 4, n).transpose(0, 1, 3, 2))
    if fmt == "e4m3":
        words = by_word.astype(ml_dtypes.float8_e4m3fn).view(np.uint8)
    else:
        c = by_word.astype(ml_dtypes.float4_e2m1fn).view(np.uint8) & 0xF
        words = c[..., 0::2] | (c[..., 1::2] << 4)
    return np.ascontiguousarray(words), np.ascontiguousarray(byte.astype(np.uint8).reshape(k // 512, 16, n))


def unpack_weight(words, scales, fmt):
    g, p, n, _ = words.shape
    if fmt == "e4m3":
        vals = np.ascontiguousarray(words).view(ml_dtypes.float8_e4m3fn).astype(np.float64)
    else:
        nib = np.empty((g, p, n, 4), np.uint8)
        nib[..., 0::2] = words & 0xF
        nib[..., 1::2] = words >> 4
        vals = E2M1[nib]
    vals = vals * np.repeat(np.exp2(scales.astype(np.float64) - 127.0), 8, axis=1)[..., None]
    return vals.transpose(0, 1, 3, 2).reshape(g * 512, n)


B, I, H, C, S = 1024, 512, 1024, 511, 3
EPSILON = 1e-6
CC = 1 + C
K = I + H
FMT = "e4m3"


def setup_inputs():
    s = mx_kscale(K)
    t = mx_kscale(CC)
    t = t / t.min()
    invariant_input = bf(np.random.standard_normal((B, I)) * s[:I])
    equivariant_input = bf(np.random.standard_normal((B, S)) * 0.125 * t[0])
    invariant_hidden = bf(np.random.standard_normal((B, H)) * s[I:])
    equivariant_hidden = bf(np.random.standard_normal((B, S, C)) * 0.125 * t[1:])
    W_left_words, W_left_scales = pack_weight(np.random.standard_normal((CC, H)) * 0.15 / np.sqrt(CC) * t[:, None], FMT)
    W_right_words, W_right_scales = pack_weight(np.random.standard_normal((CC, H)) * 0.15 / np.sqrt(CC) * t[:, None], FMT)
    W_ii_words, W_ii_scales = pack_weight(np.random.standard_normal((K, H)) * 0.6 / np.sqrt(K) / s[:, None], FMT)
    b_ii = bf(np.random.standard_normal(H) * 0.3)
    return {
        "invariant_input": invariant_input,
        "equivariant_input": equivariant_input,
        "invariant_hidden": invariant_hidden,
        "equivariant_hidden": equivariant_hidden,
        "W_left_words": W_left_words,
        "W_left_scales": W_left_scales,
        "W_right_words": W_right_words,
        "W_right_scales": W_right_scales,
        "W_ii_words": W_ii_words,
        "W_ii_scales": W_ii_scales,
        "b_ii": b_ii,
    }


def reference(invariant_input, equivariant_input, invariant_hidden, equivariant_hidden, W_left_words, W_left_scales, W_right_words, W_right_scales, W_ii_words, W_ii_scales, b_ii):
    eq_comb = np.concatenate([f64(equivariant_input)[..., None], f64(equivariant_hidden)], axis=-1)
    inv_comb = np.concatenate([f64(invariant_input), f64(invariant_hidden)], axis=-1)
    norm = np.sum(eq_comb * eq_comb, axis=-2, keepdims=True) + EPSILON
    xn = mxq(eq_comb / norm, 2, "e4m3")
    left = xn @ unpack_weight(W_left_words, W_left_scales, FMT)
    right = xn @ unpack_weight(W_right_words, W_right_scales, FMT)
    proj = np.sum(left * right, axis=-2)
    lin = mxq(inv_comb, 1, "e4m3") @ unpack_weight(W_ii_words, W_ii_scales, FMT)
    return np.tanh(proj + lin + f64(b_ii))

@@ -1,0 +1,319 @@
+from contextlib import ExitStack
+
+import concourse.mybir as mybir
+from concourse.masks import make_identity
+
+F32 = mybir.dt.float32
+BF16 = mybir.dt.bfloat16
+I32 = mybir.dt.int32
+U32 = mybir.dt.uint32
+U8 = mybir.dt.uint8
+FP8X4 = mybir.dt.float8_e4m3fn_x4
+ALU = mybir.AluOpType
+ACT = mybir.ActivationFunctionType
+
+P = 128
+TOKENS = 1024
+TILES = TOKENS // P
+PAIRS = TILES // 2
+PAIR_COLS = 2 * P
+COMPONENTS = 3
+CHANNELS = 512
+INPUT_FEATURES = 512
+FEATURES = 1536
+HIDDEN = 1024
+K_PASS = 512
+INV_PASSES = FEATURES // K_PASS
+WORDS = K_PASS // 2
+N_TILE = 512
+HALVES = HIDDEN // N_TILE
+EPSILON = 1e-6
+FILL = 16
+TURN_BANKS = 2
+MM_BANKS = 6
+STEPS = COMPONENTS * TILES
+PERIOD = 2 * COMPONENTS
+FIRST_TANH = 2 * PERIOD + 2
+FINISH_LAG = 3
+
+FLOPS = 2 * TOKENS * HIDDEN * (2 * COMPONENTS * CHANNELS + FEATURES)
+
+
+def tile_ryeelman_pa_kernel(
+    tc,
+    invariant_input,
+    equivariant_input,
+    invariant_hidden,
+    equivariant_hidden,
+    W_left_words,
+    W_left_scales,
+    W_right_words,
+    W_right_scales,
+    W_ii_words,
+    W_ii_scales,
+    b_ii,
+    out,
+):
+    nc = tc.nc
+    with ExitStack() as ctx:
+        ctx.enter_context(tc.manual_schedule())
+        keep = ctx.enter_context(tc.tile_pool(name="keep", bufs=1))
+        stage = ctx.enter_context(tc.tile_pool(name="stage", bufs=2))
+        flow = ctx.enter_context(tc.tile_pool(name="flow", bufs=3))
+        psum_turn = ctx.enter_context(tc.psum_pool(name="psum_turn", bufs=TURN_BANKS))
+        psum_mm = ctx.enter_context(tc.psum_pool(name="psum_mm", bufs=MM_BANKS))
+
+        identity = keep.tile([P, P], F32)
+        first_channel = keep.tile([P, TILES * COMPONENTS], BF16)
+        eq_sb = keep.tile([P, TILES * COMPONENTS, CHANNELS], BF16)
+        inv_sb = keep.tile([P, TILES, FEATURES], BF16)
+        bias_sb = keep.tile([P, HIDDEN], BF16)
+        w_ii = keep.tile([P, INV_PASSES, HIDDEN], U32, align_bytes=64)
+        w_left = keep.tile([P, HIDDEN], U32, align_bytes=64)
+        w_right = keep.tile([P, HIDDEN], U32, align_bytes=64)
+        w_ii_planes = keep.tile([P, HIDDEN], U8, align_bytes=64)
+        w_lr_planes = keep.tile([P, HIDDEN], U8, align_bytes=64)
+        inv_codes = keep.tile([P, INV_PASSES, TOKENS], U32, align_bytes=64)
+        inv_scales = keep.tile([P, INV_PASSES, TOKENS], U8, align_bytes=64)
+        xn_codes = keep.tile([P, COMPONENTS, TOKENS], U32, align_bytes=64)
+        xn_scales = keep.tile([P, COMPONENTS, TOKENS], U8, align_bytes=64)
+        acc = [keep.tile([P, HIDDEN], F32, name="acc%d" % t) for t in range(TILES)]
+
+        make_identity(nc, identity[:])
+        warm = keep.tile([P, 1], F32)
+        nc.vector.memset(warm[:], 1.0)
+        nc.scalar.activation(out=warm[:], in_=warm[:], func=ACT.Abs_reciprocal_sqrt)
+        nc.vector.memset(w_ii_planes[:].bitcast(I32), 0)
+        nc.vector.memset(w_lr_planes[:].bitcast(I32), 0)
+
+        nc.sync.dma_start(out=first_channel[:], in_=equivariant_input.rearrange("(p t) j -> p (t j)", t=TILES))
+        nc.vector.tensor_copy(
+            out=eq_sb[:, :, 0:FILL],
+            in_=first_channel[:].unsqueeze(2).to_broadcast([P, TILES * COMPONENTS, FILL]),
+        )
+        nc.scalar.dma_start(out=bias_sb[:], in_=b_ii.partition_broadcast(P))
+
+        hidden_vectors = equivariant_hidden.rearrange("(p t) j c -> p (t j) c", t=TILES)
+        input_features = invariant_input.rearrange("(p t) k -> p t k", t=TILES)
+        hidden_features = invariant_hidden.rearrange("(p t) k -> p t k", t=TILES)
+
+        def load_eq(q):
+            rows = slice(2 * COMPONENTS * q, 2 * COMPONENTS * (q + 1))
+            nc.sync.dma_start(out=eq_sb[:, rows, 1:CHANNELS], in_=hidden_vectors[:, rows, :])
+
+        def load_inv(q):
+            tiles = slice(2 * q, 2 * q + 2)
+            nc.sync.dma_start(out=inv_sb[:, tiles, 0:INPUT_FEATURES], in_=input_features[:, tiles, :])
+            nc.sync.dma_start(out=inv_sb[:, tiles, INPUT_FEATURES:FEATURES], in_=hidden_features[:, tiles, :])
+
+        def load_words(dst, words):
+            nc.sync.dma_start(out=dst.bitcast(I32), in_=words.rearrange("p n t -> p (n t)").bitcast(I32))
+
+        def load_w_ii():
+            for quadrant in range(4):
+                rows = slice(4 * quadrant, 4 * quadrant + 4)
+                nc.sync.dma_start(
+                    out=w_ii_planes[32 * quadrant : 32 * quadrant + 4 * INV_PASSES, :].bitcast(I32),
+                    in_=W_ii_scales[:, rows, :].bitcast(I32),
+                )
+            for g in range(INV_PASSES):
+                load_words(w_ii[:, g, :], W_ii_words[g])
+
+        def load_w_left_right():
+            for quadrant in range(4):
+                rows = slice(4 * quadrant, 4 * quadrant + 4)
+                nc.sync.dma_start(
+                    out=w_lr_planes[32 * quadrant : 32 * quadrant + 4, :].bitcast(I32),
+                    in_=W_left_scales[0, rows, :].bitcast(I32),
+                )
+                nc.sync.dma_start(
+                    out=w_lr_planes[32 * quadrant + 4 : 32 * quadrant + 8, :].bitcast(I32),
+                    in_=W_right_scales[0, rows, :].bitcast(I32),
+                )
+            load_words(w_left[:], W_left_words[0])
+            load_words(w_right[:], W_right_words[0])
+
+        load_inv(0)
+        load_eq(0)
+        load_w_ii()
+        load_eq(1)
+        load_w_left_right()
+        load_inv(1)
+        load_eq(2)
+        load_inv(2)
+        load_eq(3)
+        load_inv(3)
+
+        def transpose_pair(bank, rows_of_tile):
+            for i in range(2):
+                words = rows_of_tile(i)
+                for u in range(2):
+                    nc.tensor.transpose(bank[:, u, i * P : (i + 1) * P], words[:, u:WORDS:2], identity[:])
+
+        def as_bf16(bank):
+            return bank[:].rearrange("p u c -> p (u c)").bitcast(BF16)
+
+        def quantise_inv(q, g):
+            cols = slice(q * PAIR_COLS, (q + 1) * PAIR_COLS)
+            bank = psum_turn.tile([P, 2, PAIR_COLS], F32, tag="turn")
+            transpose_pair(bank, lambda i: inv_sb[:, 2 * q + i, g * K_PASS : (g + 1) * K_PASS].bitcast(F32))
+            grouped = flow.tile([P, PAIR_COLS, 4], BF16, tag="inv_grouped", align_bytes=64)
+            nc.scalar.copy(
+                out=grouped[:].rearrange("p c t -> p (c t)").bitcast(F32).rearrange("p (c u) -> p c u", u=2),
+                in_=bank[:].rearrange("p u c -> p c u"),
+            )
+            nc.vector.quantize_mx(
+                out=inv_codes[:, g, cols].bitcast(FP8X4),
+                scales=inv_scales[:, g, cols],
+                in_=grouped[:].rearrange("p c t -> p (c t)"),
+            )
+
+        def eq_rows(q, j):
+            return lambda i: eq_sb[:, (2 * q + i) * COMPONENTS + j, :].bitcast(F32)
+
+        squares = {}
+        recip = {}
+
+        def square(q, j):
+            if j == 0:
+                squares[q] = stage.tile([P, 2, COMPONENTS, CHANNELS], F32, name="squares")
+            first_row = 2 * COMPONENTS * q + j
+            nc.scalar.activation(
+                out=squares[q][:, :, j, :].rearrange("p i (t c) -> p i t c", t=4),
+                in_=eq_sb[:, first_row : first_row + COMPONENTS + 1 : COMPONENTS, :].rearrange(
+                    "p i (c t) -> p i t c", t=4
+                ),
+                func=ACT.Square,
+            )
+
+        norm_banks = {}
+
+        def add_squares(q):
+            for b in range(2):
+                bank = psum_turn.tile([P, 2, PAIR_COLS], F32, tag="turn")
+                for u in range(2):
+                    channels = slice((2 * b + u) * P, (2 * b + u + 1) * P)
+                    for i in range(2):
+                        for j in range(COMPONENTS):
+                            nc.tensor.matmul(
+                                out=bank[:, u, i * P : (i + 1) * P],
+                                lhsT=squares[q][:, i, j, channels],
+                                rhs=identity[:],
+                                is_transpose=True,
+                                start=(j == 0),
+                                stop=(j == COMPONENTS - 1),
+                            )
+                norm_banks[(q, b)] = bank
+
+        def reciprocal_sqrt(q):
+            recip[q] = stage.tile([P, 2, 2 * PAIR_COLS], F32, name="recip")
+            for b in range(2):
+                nc.scalar.activation(
+                    out=recip[q][:, b, :],
+                    in_=norm_banks[(q, b)][:].rearrange("p u c -> p (u c)"),
+                    func=ACT.Abs_reciprocal_sqrt,
+                    bias=EPSILON,
+                )
+
+        def reciprocal(q):
+            nc.scalar.activation(out=recip[q][:], in_=recip[q][:], func=ACT.Square)
+
+        def quantise_xn(q, j):
+            cols = slice(q * PAIR_COLS, (q + 1) * PAIR_COLS)
+            bank = psum_turn.tile([P, 2, PAIR_COLS], F32, tag="turn")
+            transpose_pair(bank, eq_rows(q, j))
+            grouped = flow.tile([P, PAIR_COLS, 2, 2], BF16, tag="xn_grouped", align_bytes=64)
+            nc.vector.tensor_tensor(
+                out=grouped[:],
+                in0=as_bf16(bank).rearrange("p (u c e) -> p c u e", u=2, e=2),
+                in1=recip[q][:].rearrange("p u (e c) -> p c u e", e=2),
+                op=ALU.mult,
+            )
+            nc.vector.quantize_mx(
+                out=xn_codes[:, j, cols].bitcast(FP8X4),
+                scales=xn_scales[:, j, cols],
+                in_=grouped[:].rearrange("p c u e -> p (c u e)"),
+            )
+
+        def linear_half(t, h):
+            tokens = slice(t * P, (t + 1) * P)
+            cols = slice(h * N_TILE, (h + 1) * N_TILE)
+            lin = psum_mm.tile([P, N_TILE], F32, tag="mm")
+            for g in range(INV_PASSES):
+                nc.tensor.matmul_mx(
+                    out=lin[:],
+                    lhsT=inv_codes[:, g, tokens].bitcast(FP8X4),
+                    lhsT_scale=inv_scales[:, g, tokens],
+                    rhs=w_ii[:, g, cols].bitcast(FP8X4),
+                    rhs_scale=w_ii_planes[4 * g : P, cols],
+                    start=(g == 0),
+                    stop=(g == INV_PASSES - 1),
+                )
+            nc.vector.tensor_tensor(out=acc[t][:, cols], in0=lin[:], in1=bias_sb[:, cols], op=ALU.add)
+
+        def products(t, j):
+            tokens = slice(t * P, (t + 1) * P)
+            product = flow.tile([P, HIDDEN], F32)
+            for h in range(HALVES):
+                cols = slice(h * N_TILE, (h + 1) * N_TILE)
+                left = psum_mm.tile([P, N_TILE], F32, tag="mm")
+                right = psum_mm.tile([P, N_TILE], F32, tag="mm")
+                for bank, words, first_row in ((left, w_left, 0), (right, w_right, 4)):
+                    nc.tensor.matmul_mx(
+                        out=bank[:],
+                        lhsT=xn_codes[:, j, tokens].bitcast(FP8X4),
+                        lhsT_scale=xn_scales[:, j, tokens],
+                        rhs=words[:, cols].bitcast(FP8X4),
+                        rhs_scale=w_lr_planes[first_row:P, cols],
+                        start=True,
+                        stop=True,
+                    )
+                left_sb = flow.tile([P, N_TILE], F32)
+                nc.scalar.copy(out=left_sb[:], in_=left[:])
+                nc.vector.tensor_tensor(out=product[:, cols], in0=left_sb[:], in1=right[:], op=ALU.mult)
+            nc.gpsimd.tensor_tensor(out=acc[t][:], in0=acc[t][:], in1=product[:], op=ALU.add)
+
+        out_tiles = out.rearrange("(p t) h -> p t h", t=TILES)
+
+        def finish(t):
+            nc.scalar.activation(out=acc[t][:], in_=acc[t][:], func=ACT.Tanh)
+            nc.sync.dma_start(out=out_tiles[:, t, :], in_=acc[t][:])
+
+        def prepare(step):
+            period = step // PERIOD
+            k = step % PERIOD
+            near = period + 1
+            far = period + 2
+            if k == 0:
+                if 0 <= near < PAIRS:
+                    for g in range(INV_PASSES):
+                        quantise_inv(near, g)
+                    add_squares(near)
+            elif k == 1:
+                if 0 <= near < PAIRS:
+                    reciprocal_sqrt(near)
+                    linear_half(2 * near, 0)
+                    linear_half(2 * near, 1)
+            elif k == 2:
+                if 0 <= near < PAIRS:
+                    reciprocal(near)
+                    linear_half(2 * near + 1, 0)
+                    linear_half(2 * near + 1, 1)
+            else:
+                if 0 <= near < PAIRS:
+                    quantise_xn(near, k - 3)
+                if 0 <= far < PAIRS:
+                    square(far, k - 3)
+
+        for step in range(-2 * PERIOD, 0):
+            prepare(step)
+        finished = []
+        for step in range(STEPS):
+            products(step // COMPONENTS, step % COMPONENTS)
+            prepare(step)
+            t = len(finished)
+            if step >= FIRST_TANH and step >= COMPONENTS * t + COMPONENTS - 1 + FINISH_LAG:
+                finish(t)
+                finished.append(t)
+        for t in range(len(finished), TILES):
+            finish(t)

@@ -29,6 +29,7 @@ N_TILE = 512
 HALVES = HIDDEN // N_TILE
 EPSILON = 1e-6
 FILL = 16
+VECTOR_ADDS = 1
 TURN_BANKS = 2
 MM_BANKS = 6
 STEPS = COMPONENTS * TILES
@@ -271,7 +272,8 @@ def tile_ryeelman_pa_kernel(
                 left_sb = flow.tile([P, N_TILE], F32)
                 nc.scalar.copy(out=left_sb[:], in_=left[:])
                 nc.vector.tensor_tensor(out=product[:, cols], in0=left_sb[:], in1=right[:], op=ALU.mult)
-            nc.gpsimd.tensor_tensor(out=acc[t][:], in0=acc[t][:], in1=product[:], op=ALU.add)
+            adder = nc.vector if j < VECTOR_ADDS else nc.gpsimd
+            adder.tensor_tensor(out=acc[t][:], in0=acc[t][:], in1=product[:], op=ALU.add)
 
         out_tiles = out.rearrange("(p t) h -> p t h", t=TILES)
 

@@ -15,27 +15,32 @@ ACT = mybir.ActivationFunctionType
 P = 128
 TOKENS = 1024
 TILES = TOKENS // P
-PAIRS = TILES // 2
-PAIR_COLS = 2 * P
 COMPONENTS = 3
 CHANNELS = 512
 INPUT_FEATURES = 512
 FEATURES = 1536
 HIDDEN = 1024
 K_PASS = 512
+PACK = 4
 INV_PASSES = FEATURES // K_PASS
 WORDS = K_PASS // 2
 N_TILE = 512
 HALVES = HIDDEN // N_TILE
 EPSILON = 1e-6
 FILL = 16
-VECTOR_ADDS = 1
-TURN_BANKS = 2
-MM_BANKS = 6
+LOAD_TILES = 2
+FLOW_BUFS = 4
+TURN_BANKS = 3
+LEFT_BANKS = 2
+RIGHT_BANKS = 3
+
+SQUARE_AHEAD = 3
+RECIPROCAL_AHEAD = 2
+XN_AHEAD = 1
+LINEAR_BEHIND = 1
+TOTAL_BEHIND = 2
 STEPS = COMPONENTS * TILES
-PERIOD = 2 * COMPONENTS
-FIRST_TANH = 2 * PERIOD + 2
-FINISH_LAG = 3
+FIRST_TANH = COMPONENTS * (TILES - 1 - RECIPROCAL_AHEAD) + 1
 
 FLOPS = 2 * TOKENS * HIDDEN * (2 * COMPONENTS * CHANNELS + FEATURES)
 
@@ -59,10 +64,10 @@ def tile_ryeelman_pa_kernel(
     with ExitStack() as ctx:
         ctx.enter_context(tc.manual_schedule())
         keep = ctx.enter_context(tc.tile_pool(name="keep", bufs=1))
-        stage = ctx.enter_context(tc.tile_pool(name="stage", bufs=2))
-        flow = ctx.enter_context(tc.tile_pool(name="flow", bufs=3))
+        flow = ctx.enter_context(tc.tile_pool(name="flow", bufs=FLOW_BUFS))
         psum_turn = ctx.enter_context(tc.psum_pool(name="psum_turn", bufs=TURN_BANKS))
-        psum_mm = ctx.enter_context(tc.psum_pool(name="psum_mm", bufs=MM_BANKS))
+        psum_left = ctx.enter_context(tc.psum_pool(name="psum_left", bufs=LEFT_BANKS))
+        psum_right = ctx.enter_context(tc.psum_pool(name="psum_right", bufs=RIGHT_BANKS))
 
         identity = keep.tile([P, P], F32)
         first_channel = keep.tile([P, TILES * COMPONENTS], BF16)
@@ -99,28 +104,30 @@ def tile_ryeelman_pa_kernel(
         hidden_features = invariant_hidden.rearrange("(p t) k -> p t k", t=TILES)
 
         def load_eq(q):
-            rows = slice(2 * COMPONENTS * q, 2 * COMPONENTS * (q + 1))
+            rows = slice(LOAD_TILES * COMPONENTS * q, LOAD_TILES * COMPONENTS * (q + 1))
             nc.sync.dma_start(out=eq_sb[:, rows, 1:CHANNELS], in_=hidden_vectors[:, rows, :])
 
         def load_inv(q):
-            tiles = slice(2 * q, 2 * q + 2)
+            tiles = slice(LOAD_TILES * q, LOAD_TILES * (q + 1))
             nc.sync.dma_start(out=inv_sb[:, tiles, 0:INPUT_FEATURES], in_=input_features[:, tiles, :])
             nc.sync.dma_start(out=inv_sb[:, tiles, INPUT_FEATURES:FEATURES], in_=hidden_features[:, tiles, :])
 
         def load_words(dst, words):
             nc.sync.dma_start(out=dst.bitcast(I32), in_=words.rearrange("p n t -> p (n t)").bitcast(I32))
 
-        def load_w_ii():
+        def load_w_ii_scales():
             for quadrant in range(4):
                 rows = slice(4 * quadrant, 4 * quadrant + 4)
                 nc.sync.dma_start(
                     out=w_ii_planes[32 * quadrant : 32 * quadrant + 4 * INV_PASSES, :].bitcast(I32),
                     in_=W_ii_scales[:, rows, :].bitcast(I32),
                 )
+
+        def load_w_ii_words():
             for g in range(INV_PASSES):
                 load_words(w_ii[:, g, :], W_ii_words[g])
 
-        def load_w_left_right():
+        def load_w_left_right_scales():
             for quadrant in range(4):
                 rows = slice(4 * quadrant, 4 * quadrant + 4)
                 nc.sync.dma_start(
@@ -131,115 +138,103 @@ def tile_ryeelman_pa_kernel(
                     out=w_lr_planes[32 * quadrant + 4 : 32 * quadrant + 8, :].bitcast(I32),
                     in_=W_right_scales[0, rows, :].bitcast(I32),
                 )
+
+        def load_w_left_right_words():
             load_words(w_left[:], W_left_words[0])
             load_words(w_right[:], W_right_words[0])
 
-        load_inv(0)
+        load_w_left_right_words()
         load_eq(0)
-        load_w_ii()
         load_eq(1)
-        load_w_left_right()
-        load_inv(1)
+        load_w_left_right_scales()
+        load_inv(0)
+        load_w_ii_scales()
+        load_w_ii_words()
         load_eq(2)
-        load_inv(2)
+        load_inv(1)
         load_eq(3)
+        load_inv(2)
         load_inv(3)
 
-        def transpose_pair(bank, rows_of_tile):
-            for i in range(2):
-                words = rows_of_tile(i)
-                for u in range(2):
-                    nc.tensor.transpose(bank[:, u, i * P : (i + 1) * P], words[:, u:WORDS:2], identity[:])
+        def transpose_words(words):
+            bank = psum_turn.tile([P, 2, P], F32, tag="turn")
+            for u in range(2):
+                nc.tensor.transpose(bank[:, u, :], words[:, u:WORDS:2], identity[:])
+            return bank
 
-        def as_bf16(bank):
-            return bank[:].rearrange("p u c -> p (u c)").bitcast(BF16)
-
-        def quantise_inv(q, g):
-            cols = slice(q * PAIR_COLS, (q + 1) * PAIR_COLS)
-            bank = psum_turn.tile([P, 2, PAIR_COLS], F32, tag="turn")
-            transpose_pair(bank, lambda i: inv_sb[:, 2 * q + i, g * K_PASS : (g + 1) * K_PASS].bitcast(F32))
-            grouped = flow.tile([P, PAIR_COLS, 4], BF16, tag="inv_grouped", align_bytes=64)
+        def quantise_inv(t, g):
+            bank = transpose_words(inv_sb[:, t, g * K_PASS : (g + 1) * K_PASS].bitcast(F32))
+            grouped = flow.tile([P, P, PACK], BF16, tag="inv_grouped", align_bytes=64)
             nc.scalar.copy(
                 out=grouped[:].rearrange("p c t -> p (c t)").bitcast(F32).rearrange("p (c u) -> p c u", u=2),
                 in_=bank[:].rearrange("p u c -> p c u"),
             )
             nc.vector.quantize_mx(
-                out=inv_codes[:, g, cols].bitcast(FP8X4),
-                scales=inv_scales[:, g, cols],
+                out=inv_codes[:, g, t * P : (t + 1) * P].bitcast(FP8X4),
+                scales=inv_scales[:, g, t * P : (t + 1) * P],
                 in_=grouped[:].rearrange("p c t -> p (c t)"),
             )
 
-        def eq_rows(q, j):
-            return lambda i: eq_sb[:, (2 * q + i) * COMPONENTS + j, :].bitcast(F32)
-
         squares = {}
+        sums = {}
         recip = {}
+        grouped_xn = {}
 
-        def square(q, j):
+        def square(t, j):
             if j == 0:
-                squares[q] = stage.tile([P, 2, COMPONENTS, CHANNELS], F32, name="squares")
-            first_row = 2 * COMPONENTS * q + j
+                squares[t] = flow.tile([P, COMPONENTS, CHANNELS], F32, name="squares")
             nc.scalar.activation(
-                out=squares[q][:, :, j, :].rearrange("p i (t c) -> p i t c", t=4),
-                in_=eq_sb[:, first_row : first_row + COMPONENTS + 1 : COMPONENTS, :].rearrange(
-                    "p i (c t) -> p i t c", t=4
-                ),
+                out=squares[t][:, j, :].rearrange("p (r c) -> p r c", r=PACK),
+                in_=eq_sb[:, COMPONENTS * t + j, :].rearrange("p (c r) -> p r c", r=PACK),
                 func=ACT.Square,
             )
 
-        norm_banks = {}
+        def add_squares(t):
+            sums[t] = psum_turn.tile([P, PACK, P], F32, tag="turn", name="sums")
+            for r in range(PACK):
+                for j in range(COMPONENTS):
+                    nc.tensor.matmul(
+                        out=sums[t][:, r, :],
+                        lhsT=squares[t][:, j, r * P : (r + 1) * P],
+                        rhs=identity[:],
+                        is_transpose=True,
+                        start=(j == 0),
+                        stop=(j == COMPONENTS - 1),
+                    )
 
-        def add_squares(q):
-            for b in range(2):
-                bank = psum_turn.tile([P, 2, PAIR_COLS], F32, tag="turn")
-                for u in range(2):
-                    channels = slice((2 * b + u) * P, (2 * b + u + 1) * P)
-                    for i in range(2):
-                        for j in range(COMPONENTS):
-                            nc.tensor.matmul(
-                                out=bank[:, u, i * P : (i + 1) * P],
-                                lhsT=squares[q][:, i, j, channels],
-                                rhs=identity[:],
-                                is_transpose=True,
-                                start=(j == 0),
-                                stop=(j == COMPONENTS - 1),
-                            )
-                norm_banks[(q, b)] = bank
+        def reciprocal_sqrt(t):
+            recip[t] = flow.tile([P, CHANNELS], F32, name="recip")
+            nc.scalar.activation(
+                out=recip[t][:],
+                in_=sums[t][:].rearrange("p r c -> p (r c)"),
+                func=ACT.Abs_reciprocal_sqrt,
+                bias=EPSILON,
+            )
 
-        def reciprocal_sqrt(q):
-            recip[q] = stage.tile([P, 2, 2 * PAIR_COLS], F32, name="recip")
-            for b in range(2):
-                nc.scalar.activation(
-                    out=recip[q][:, b, :],
-                    in_=norm_banks[(q, b)][:].rearrange("p u c -> p (u c)"),
-                    func=ACT.Abs_reciprocal_sqrt,
-                    bias=EPSILON,
-                )
+        def reciprocal(t):
+            nc.scalar.activation(out=recip[t][:], in_=recip[t][:], func=ACT.Square)
 
-        def reciprocal(q):
-            nc.scalar.activation(out=recip[q][:], in_=recip[q][:], func=ACT.Square)
-
-        def quantise_xn(q, j):
-            cols = slice(q * PAIR_COLS, (q + 1) * PAIR_COLS)
-            bank = psum_turn.tile([P, 2, PAIR_COLS], F32, tag="turn")
-            transpose_pair(bank, eq_rows(q, j))
-            grouped = flow.tile([P, PAIR_COLS, 2, 2], BF16, tag="xn_grouped", align_bytes=64)
+        def scale_xn(t, j):
+            bank = transpose_words(eq_sb[:, COMPONENTS * t + j, :].bitcast(F32))
+            grouped_xn[(t, j)] = flow.tile([P, P, 2, 2], BF16, name="grouped_xn", align_bytes=64)
             nc.vector.tensor_tensor(
-                out=grouped[:],
-                in0=as_bf16(bank).rearrange("p (u c e) -> p c u e", u=2, e=2),
-                in1=recip[q][:].rearrange("p u (e c) -> p c u e", e=2),
+                out=grouped_xn[(t, j)][:],
+                in0=bank[:].rearrange("p u c -> p (u c)").bitcast(BF16).rearrange("p (u c e) -> p c u e", u=2, e=2),
+                in1=recip[t][:].rearrange("p (u e c) -> p c u e", u=2, e=2),
                 op=ALU.mult,
             )
+
+        def quantise_xn(t, j):
             nc.vector.quantize_mx(
-                out=xn_codes[:, j, cols].bitcast(FP8X4),
-                scales=xn_scales[:, j, cols],
-                in_=grouped[:].rearrange("p c u e -> p (c u e)"),
+                out=xn_codes[:, j, t * P : (t + 1) * P].bitcast(FP8X4),
+                scales=xn_scales[:, j, t * P : (t + 1) * P],
+                in_=grouped_xn[(t, j)][:].rearrange("p c u e -> p (c u e)"),
             )
 
         def linear_half(t, h):
             tokens = slice(t * P, (t + 1) * P)
             cols = slice(h * N_TILE, (h + 1) * N_TILE)
-            lin = psum_mm.tile([P, N_TILE], F32, tag="mm")
+            lin = psum_right.tile([P, N_TILE], F32, tag="right")
             for g in range(INV_PASSES):
                 nc.tensor.matmul_mx(
                     out=lin[:],
@@ -250,30 +245,45 @@ def tile_ryeelman_pa_kernel(
                     start=(g == 0),
                     stop=(g == INV_PASSES - 1),
                 )
-            nc.vector.tensor_tensor(out=acc[t][:, cols], in0=lin[:], in1=bias_sb[:, cols], op=ALU.add)
+            nc.vector.tensor_tensor(out=last_product[t][:, cols], in0=lin[:], in1=last_product[t][:, cols], op=ALU.add)
+
+        def project(bank, t, j, h, words, first_row):
+            cols = slice(h * N_TILE, (h + 1) * N_TILE)
+            nc.tensor.matmul_mx(
+                out=bank[:],
+                lhsT=xn_codes[:, j, t * P : (t + 1) * P].bitcast(FP8X4),
+                lhsT_scale=xn_scales[:, j, t * P : (t + 1) * P],
+                rhs=words[:, cols].bitcast(FP8X4),
+                rhs_scale=w_lr_planes[first_row:P, cols],
+                start=True,
+                stop=True,
+            )
+
+        last_product = {}
 
         def products(t, j):
-            tokens = slice(t * P, (t + 1) * P)
-            product = flow.tile([P, HIDDEN], F32)
+            lefts = [psum_left.tile([P, N_TILE], F32, tag="left", name="left%d" % h) for h in range(HALVES)]
             for h in range(HALVES):
-                cols = slice(h * N_TILE, (h + 1) * N_TILE)
-                left = psum_mm.tile([P, N_TILE], F32, tag="mm")
-                right = psum_mm.tile([P, N_TILE], F32, tag="mm")
-                for bank, words, first_row in ((left, w_left, 0), (right, w_right, 4)):
-                    nc.tensor.matmul_mx(
-                        out=bank[:],
-                        lhsT=xn_codes[:, j, tokens].bitcast(FP8X4),
-                        lhsT_scale=xn_scales[:, j, tokens],
-                        rhs=words[:, cols].bitcast(FP8X4),
-                        rhs_scale=w_lr_planes[first_row:P, cols],
-                        start=True,
-                        stop=True,
-                    )
+                project(lefts[h], t, j, h, w_left, 0)
+            rights = [psum_right.tile([P, N_TILE], F32, tag="right", name="right%d" % h) for h in range(HALVES)]
+            for h in range(HALVES):
+                project(rights[h], t, j, h, w_right, 4)
+            product = flow.tile([P, HIDDEN], F32, name="product", tag="product" if j < COMPONENTS - 1 else "last_product")
+            for h in range(HALVES):
                 left_sb = flow.tile([P, N_TILE], F32)
-                nc.scalar.copy(out=left_sb[:], in_=left[:])
-                nc.vector.tensor_tensor(out=product[:, cols], in0=left_sb[:], in1=right[:], op=ALU.mult)
-            adder = nc.vector if j < VECTOR_ADDS else nc.gpsimd
-            adder.tensor_tensor(out=acc[t][:], in0=acc[t][:], in1=product[:], op=ALU.add)
+                nc.scalar.copy(out=left_sb[:], in_=lefts[h][:])
+                nc.vector.tensor_tensor(
+                    out=product[:, h * N_TILE : (h + 1) * N_TILE], in0=left_sb[:], in1=rights[h][:], op=ALU.mult
+                )
+            if j == 0:
+                nc.gpsimd.tensor_tensor(out=acc[t][:], in0=product[:], in1=bias_sb[:], op=ALU.add)
+            elif j == 1:
+                nc.gpsimd.tensor_tensor(out=acc[t][:], in0=acc[t][:], in1=product[:], op=ALU.add)
+            else:
+                last_product[t] = product
+
+        def total(t):
+            nc.gpsimd.tensor_tensor(out=acc[t][:], in0=acc[t][:], in1=last_product[t][:], op=ALU.add)
 
         out_tiles = out.rearrange("(p t) h -> p t h", t=TILES)
 
@@ -281,41 +291,34 @@ def tile_ryeelman_pa_kernel(
             nc.scalar.activation(out=acc[t][:], in_=acc[t][:], func=ACT.Tanh)
             nc.sync.dma_start(out=out_tiles[:, t, :], in_=acc[t][:])
 
-        def prepare(step):
-            period = step // PERIOD
-            k = step % PERIOD
-            near = period + 1
-            far = period + 2
-            if k == 0:
-                if 0 <= near < PAIRS:
-                    for g in range(INV_PASSES):
-                        quantise_inv(near, g)
-                    add_squares(near)
-            elif k == 1:
-                if 0 <= near < PAIRS:
-                    reciprocal_sqrt(near)
-                    linear_half(2 * near, 0)
-                    linear_half(2 * near, 1)
-            elif k == 2:
-                if 0 <= near < PAIRS:
-                    reciprocal(near)
-                    linear_half(2 * near + 1, 0)
-                    linear_half(2 * near + 1, 1)
-            else:
-                if 0 <= near < PAIRS:
-                    quantise_xn(near, k - 3)
-                if 0 <= far < PAIRS:
-                    square(far, k - 3)
+        def exists(t):
+            return 0 <= t < TILES
 
-        for step in range(-2 * PERIOD, 0):
-            prepare(step)
         finished = []
-        for step in range(STEPS):
-            products(step // COMPONENTS, step % COMPONENTS)
-            prepare(step)
-            t = len(finished)
-            if step >= FIRST_TANH and step >= COMPONENTS * t + COMPONENTS - 1 + FINISH_LAG:
-                finish(t)
-                finished.append(t)
-        for t in range(len(finished), TILES):
-            finish(t)
+        for step in range(-COMPONENTS * SQUARE_AHEAD, STEPS + COMPONENTS * TOTAL_BEHIND + 1):
+            t, j = divmod(step, COMPONENTS)
+            if exists(t):
+                products(t, j)
+            if exists(t - LINEAR_BEHIND) and j > 0:
+                linear_half(t - LINEAR_BEHIND, j - 1)
+            if exists(t - TOTAL_BEHIND) and j == 0:
+                total(t - TOTAL_BEHIND)
+            earlier_t, earlier_j = divmod(step - 1, COMPONENTS)
+            if exists(earlier_t + XN_AHEAD):
+                quantise_xn(earlier_t + XN_AHEAD, earlier_j)
+            if exists(t + XN_AHEAD):
+                scale_xn(t + XN_AHEAD, j)
+            if exists(t):
+                quantise_inv(t, j)
+            if exists(t + RECIPROCAL_AHEAD):
+                if j == 0:
+                    add_squares(t + RECIPROCAL_AHEAD)
+                elif j == 1:
+                    reciprocal_sqrt(t + RECIPROCAL_AHEAD)
+                else:
+                    reciprocal(t + RECIPROCAL_AHEAD)
+            if exists(t + SQUARE_AHEAD):
+                square(t + SQUARE_AHEAD, j)
+            if step >= FIRST_TANH and len(finished) <= min(t - TOTAL_BEHIND, TILES - 1):
+                finish(len(finished))
+                finished.append(step)

@@ -30,17 +30,20 @@ EPSILON = 1e-6
 FILL = 16
 LOAD_TILES = 2
 FLOW_BUFS = 4
+COPY_BUFS = 6
 TURN_BANKS = 3
 LEFT_BANKS = 2
 RIGHT_BANKS = 3
 
-SQUARE_AHEAD = 3
-RECIPROCAL_AHEAD = 2
-XN_AHEAD = 1
+SQUARE_AHEAD = 4
+RECIPROCAL_AHEAD = 3
+XN_AHEAD = 2
+LEFT_AHEAD = 1
 LINEAR_BEHIND = 1
 TOTAL_BEHIND = 2
 STEPS = COMPONENTS * TILES
 FIRST_TANH = COMPONENTS * (TILES - 1 - RECIPROCAL_AHEAD) + 1
+FINISH_LAG = 2
 
 FLOPS = 2 * TOKENS * HIDDEN * (2 * COMPONENTS * CHANNELS + FEATURES)
 
@@ -65,6 +68,7 @@ def tile_ryeelman_pa_kernel(
         ctx.enter_context(tc.manual_schedule())
         keep = ctx.enter_context(tc.tile_pool(name="keep", bufs=1))
         flow = ctx.enter_context(tc.tile_pool(name="flow", bufs=FLOW_BUFS))
+        copies = ctx.enter_context(tc.tile_pool(name="copies", bufs=COPY_BUFS))
         psum_turn = ctx.enter_context(tc.psum_pool(name="psum_turn", bufs=TURN_BANKS))
         psum_left = ctx.enter_context(tc.psum_pool(name="psum_left", bufs=LEFT_BANKS))
         psum_right = ctx.enter_context(tc.psum_pool(name="psum_right", bufs=RIGHT_BANKS))
@@ -162,8 +166,13 @@ def tile_ryeelman_pa_kernel(
                 nc.tensor.transpose(bank[:, u, :], words[:, u:WORDS:2], identity[:])
             return bank
 
+        turned_inv = {}
+
+        def turn_inv(t, g):
+            turned_inv[(t, g)] = transpose_words(inv_sb[:, t, g * K_PASS : (g + 1) * K_PASS].bitcast(F32))
+
         def quantise_inv(t, g):
-            bank = transpose_words(inv_sb[:, t, g * K_PASS : (g + 1) * K_PASS].bitcast(F32))
+            bank = turned_inv[(t, g)]
             grouped = flow.tile([P, P, PACK], BF16, tag="inv_grouped", align_bytes=64)
             nc.scalar.copy(
                 out=grouped[:].rearrange("p c t -> p (c t)").bitcast(F32).rearrange("p (c u) -> p c u", u=2),
@@ -261,19 +270,22 @@ def tile_ryeelman_pa_kernel(
 
         last_product = {}
 
+        left_copies = {}
+
+        def lefts(t, j):
+            for h in range(HALVES):
+                left = psum_left.tile([P, N_TILE], F32, tag="left")
+                project(left, t, j, h, w_left, 0)
+                left_copies[(t, j, h)] = copies.tile([P, N_TILE], F32, name="left_sb")
+                nc.scalar.copy(out=left_copies[(t, j, h)][:], in_=left[:])
+
         def products(t, j):
-            lefts = [psum_left.tile([P, N_TILE], F32, tag="left", name="left%d" % h) for h in range(HALVES)]
-            for h in range(HALVES):
-                project(lefts[h], t, j, h, w_left, 0)
-            rights = [psum_right.tile([P, N_TILE], F32, tag="right", name="right%d" % h) for h in range(HALVES)]
-            for h in range(HALVES):
-                project(rights[h], t, j, h, w_right, 4)
             product = flow.tile([P, HIDDEN], F32, name="product", tag="product" if j < COMPONENTS - 1 else "last_product")
             for h in range(HALVES):
-                left_sb = flow.tile([P, N_TILE], F32)
-                nc.scalar.copy(out=left_sb[:], in_=lefts[h][:])
+                right = psum_right.tile([P, N_TILE], F32, tag="right")
+                project(right, t, j, h, w_right, 4)
                 nc.vector.tensor_tensor(
-                    out=product[:, h * N_TILE : (h + 1) * N_TILE], in0=left_sb[:], in1=rights[h][:], op=ALU.mult
+                    out=product[:, h * N_TILE : (h + 1) * N_TILE], in0=left_copies[(t, j, h)][:], in1=right[:], op=ALU.mult
                 )
             if j == 0:
                 nc.gpsimd.tensor_tensor(out=acc[t][:], in0=product[:], in1=bias_sb[:], op=ALU.add)
@@ -283,7 +295,7 @@ def tile_ryeelman_pa_kernel(
                 last_product[t] = product
 
         def total(t):
-            nc.gpsimd.tensor_tensor(out=acc[t][:], in0=acc[t][:], in1=last_product[t][:], op=ALU.add)
+            nc.vector.tensor_tensor(out=acc[t][:], in0=acc[t][:], in1=last_product[t][:], op=ALU.add)
 
         out_tiles = out.rearrange("(p t) h -> p t h", t=TILES)
 
@@ -295,10 +307,21 @@ def tile_ryeelman_pa_kernel(
             return 0 <= t < TILES
 
         finished = []
-        for step in range(-COMPONENTS * SQUARE_AHEAD, STEPS + COMPONENTS * TOTAL_BEHIND + 1):
+        for step in range(-COMPONENTS * SQUARE_AHEAD, STEPS + COMPONENTS * TOTAL_BEHIND + FINISH_LAG + 1):
             t, j = divmod(step, COMPONENTS)
+            later_t, later_j = divmod(step + LEFT_AHEAD, COMPONENTS)
+            if exists(later_t):
+                lefts(later_t, later_j)
             if exists(t):
                 products(t, j)
+            if exists(t + XN_AHEAD):
+                scale_xn(t + XN_AHEAD, j)
+            if exists(t):
+                turn_inv(t, j)
+            if exists(t + SQUARE_AHEAD):
+                square(t + SQUARE_AHEAD, j)
+            if exists(t + RECIPROCAL_AHEAD) and j == 0:
+                add_squares(t + RECIPROCAL_AHEAD)
             if exists(t - LINEAR_BEHIND) and j > 0:
                 linear_half(t - LINEAR_BEHIND, j - 1)
             if exists(t - TOTAL_BEHIND) and j == 0:
@@ -306,19 +329,12 @@ def tile_ryeelman_pa_kernel(
             earlier_t, earlier_j = divmod(step - 1, COMPONENTS)
             if exists(earlier_t + XN_AHEAD):
                 quantise_xn(earlier_t + XN_AHEAD, earlier_j)
-            if exists(t + XN_AHEAD):
-                scale_xn(t + XN_AHEAD, j)
+            if exists(t + RECIPROCAL_AHEAD) and j == 1:
+                reciprocal_sqrt(t + RECIPROCAL_AHEAD)
+            if exists(t + RECIPROCAL_AHEAD) and j == 2:
+                reciprocal(t + RECIPROCAL_AHEAD)
             if exists(t):
                 quantise_inv(t, j)
-            if exists(t + RECIPROCAL_AHEAD):
-                if j == 0:
-                    add_squares(t + RECIPROCAL_AHEAD)
-                elif j == 1:
-                    reciprocal_sqrt(t + RECIPROCAL_AHEAD)
-                else:
-                    reciprocal(t + RECIPROCAL_AHEAD)
-            if exists(t + SQUARE_AHEAD):
-                square(t + SQUARE_AHEAD, j)
-            if step >= FIRST_TANH and len(finished) <= min(t - TOTAL_BEHIND, TILES - 1):
+            if step >= FIRST_TANH and len(finished) < TILES and step >= COMPONENTS * (len(finished) + TOTAL_BEHIND) + FINISH_LAG:
                 finish(len(finished))
                 finished.append(step)

@@ -77,6 +77,8 @@ def tile_ryeelman_pa_kernel(
         first_channel = keep.tile([P, TILES * COMPONENTS], BF16)
         eq_sb = keep.tile([P, TILES * COMPONENTS, CHANNELS], BF16)
         inv_sb = keep.tile([P, TILES, FEATURES], BF16)
+        bias_row = keep.tile([P, HIDDEN], BF16)
+        ones = keep.tile([P, P], BF16)
         bias_sb = keep.tile([P, HIDDEN], BF16)
         w_ii = keep.tile([P, INV_PASSES, HIDDEN], U32, align_bytes=64)
         w_left = keep.tile([P, HIDDEN], U32, align_bytes=64)
@@ -95,13 +97,14 @@ def tile_ryeelman_pa_kernel(
         nc.scalar.activation(out=warm[:], in_=warm[:], func=ACT.Abs_reciprocal_sqrt)
         nc.vector.memset(w_ii_planes[:].bitcast(I32), 0)
         nc.vector.memset(w_lr_planes[:].bitcast(I32), 0)
+        nc.vector.memset(bias_row[:].bitcast(I32), 0)
+        nc.vector.memset(ones[:], 1.0)
 
         nc.sync.dma_start(out=first_channel[:], in_=equivariant_input.rearrange("(p t) j -> p (t j)", t=TILES))
         nc.vector.tensor_copy(
             out=eq_sb[:, :, 0:FILL],
             in_=first_channel[:].unsqueeze(2).to_broadcast([P, TILES * COMPONENTS, FILL]),
         )
-        nc.scalar.dma_start(out=bias_sb[:], in_=b_ii.partition_broadcast(P))
 
         hidden_vectors = equivariant_hidden.rearrange("(p t) j c -> p (t j) c", t=TILES)
         input_features = invariant_input.rearrange("(p t) k -> p t k", t=TILES)
@@ -122,9 +125,9 @@ def tile_ryeelman_pa_kernel(
         def load_w_ii_scales():
             for quadrant in range(4):
                 rows = slice(4 * quadrant, 4 * quadrant + 4)
-                nc.sync.dma_start(
-                    out=w_ii_planes[32 * quadrant : 32 * quadrant + 4 * INV_PASSES, :].bitcast(I32),
-                    in_=W_ii_scales[:, rows, :].bitcast(I32),
+                nc.gpsimd.dma_start(
+                    out=w_ii_planes[32 * quadrant : 32 * quadrant + 4 * INV_PASSES, :].bitcast(F32),
+                    in_=W_ii_scales[:, rows, :].bitcast(F32),
                 )
 
         def load_w_ii_words():
@@ -134,31 +137,38 @@ def tile_ryeelman_pa_kernel(
         def load_w_left_right_scales():
             for quadrant in range(4):
                 rows = slice(4 * quadrant, 4 * quadrant + 4)
-                nc.sync.dma_start(
-                    out=w_lr_planes[32 * quadrant : 32 * quadrant + 4, :].bitcast(I32),
-                    in_=W_left_scales[0, rows, :].bitcast(I32),
+                nc.gpsimd.dma_start(
+                    out=w_lr_planes[32 * quadrant : 32 * quadrant + 4, :].bitcast(F32),
+                    in_=W_left_scales[0, rows, :].bitcast(F32),
                 )
-                nc.sync.dma_start(
-                    out=w_lr_planes[32 * quadrant + 4 : 32 * quadrant + 8, :].bitcast(I32),
-                    in_=W_right_scales[0, rows, :].bitcast(I32),
+                nc.gpsimd.dma_start(
+                    out=w_lr_planes[32 * quadrant + 4 : 32 * quadrant + 8, :].bitcast(F32),
+                    in_=W_right_scales[0, rows, :].bitcast(F32),
                 )
 
         def load_w_left_right_words():
             load_words(w_left[:], W_left_words[0])
             load_words(w_right[:], W_right_words[0])
 
+        load_w_left_right_scales()
+        load_w_ii_scales()
+        nc.sync.dma_start(out=bias_row[0:1, :], in_=b_ii.rearrange("(o h) -> o h", o=1))
         load_w_left_right_words()
         load_eq(0)
         load_eq(1)
-        load_w_left_right_scales()
         load_inv(0)
-        load_w_ii_scales()
         load_w_ii_words()
         load_eq(2)
         load_inv(1)
         load_eq(3)
         load_inv(2)
         load_inv(3)
+
+        for h in range(HALVES):
+            cols = slice(h * N_TILE, (h + 1) * N_TILE)
+            spread = psum_right.tile([P, N_TILE], F32, tag="right")
+            nc.tensor.matmul(out=spread[:], lhsT=ones[:], rhs=bias_row[:, cols], start=True, stop=True)
+            nc.scalar.copy(out=bias_sb[:, cols], in_=spread[:])
 
         def transpose_words(words):
             bank = psum_turn.tile([P, 2, P], F32, tag="turn")

@@ -112,7 +112,8 @@ def tile_ryeelman_pa_kernel(
 
         def load_eq(q):
             rows = slice(LOAD_TILES * COMPONENTS * q, LOAD_TILES * COMPONENTS * (q + 1))
-            nc.sync.dma_start(out=eq_sb[:, rows, 1:CHANNELS], in_=hidden_vectors[:, rows, :])
+            nc.sync.dma_start(out=eq_sb[:, rows, FILL:CHANNELS], in_=hidden_vectors[:, rows, FILL - 1 :])
+            nc.sync.dma_start(out=eq_sb[:, rows, 1:FILL], in_=hidden_vectors[:, rows, 0 : FILL - 1])
 
         def load_inv(q):
             tiles = slice(LOAD_TILES * q, LOAD_TILES * (q + 1))
@@ -153,9 +154,9 @@ def tile_ryeelman_pa_kernel(
         load_w_left_right_scales()
         load_w_ii_scales()
         nc.sync.dma_start(out=bias_row[0:1, :], in_=b_ii.rearrange("(o h) -> o h", o=1))
-        load_w_left_right_words()
         load_eq(0)
         load_eq(1)
+        load_w_left_right_words()
         load_inv(0)
         load_w_ii_words()
         load_eq(2)
@@ -305,13 +306,17 @@ def tile_ryeelman_pa_kernel(
                 last_product[t] = product
 
         def total(t):
-            nc.vector.tensor_tensor(out=acc[t][:], in0=acc[t][:], in1=last_product[t][:], op=ALU.add)
+            for h in range(HALVES):
+                cols = slice(h * N_TILE, (h + 1) * N_TILE)
+                nc.vector.tensor_tensor(out=acc[t][:, cols], in0=acc[t][:, cols], in1=last_product[t][:, cols], op=ALU.add)
 
         out_tiles = out.rearrange("(p t) h -> p t h", t=TILES)
 
         def finish(t):
-            nc.scalar.activation(out=acc[t][:], in_=acc[t][:], func=ACT.Tanh)
-            nc.sync.dma_start(out=out_tiles[:, t, :], in_=acc[t][:])
+            for h in range(HALVES):
+                cols = slice(h * N_TILE, (h + 1) * N_TILE)
+                nc.scalar.activation(out=acc[t][:, cols], in_=acc[t][:, cols], func=ACT.Tanh)
+                nc.sync.dma_start(out=out_tiles[:, t, cols], in_=acc[t][:, cols])
 
         def exists(t):
             return 0 <= t < TILES

@@ -75,6 +75,7 @@ def tile_ryeelman_pa_kernel(
 
         identity = keep.tile([P, P], F32)
         first_channel = keep.tile([P, TILES * COMPONENTS], BF16)
+        first_hidden = keep.tile([P, TILES * COMPONENTS, FILL], BF16)
         eq_sb = keep.tile([P, TILES * COMPONENTS, CHANNELS], BF16)
         inv_sb = keep.tile([P, TILES, FEATURES], BF16)
         bias_row = keep.tile([P, HIDDEN], BF16)
@@ -101,10 +102,7 @@ def tile_ryeelman_pa_kernel(
         nc.vector.memset(ones[:], 1.0)
 
         nc.sync.dma_start(out=first_channel[:], in_=equivariant_input.rearrange("(p t) j -> p (t j)", t=TILES))
-        nc.vector.tensor_copy(
-            out=eq_sb[:, :, 0:FILL],
-            in_=first_channel[:].unsqueeze(2).to_broadcast([P, TILES * COMPONENTS, FILL]),
-        )
+        nc.vector.tensor_copy(out=eq_sb[:, :, 0:1], in_=first_channel[:].unsqueeze(2))
 
         hidden_vectors = equivariant_hidden.rearrange("(p t) j c -> p (t j) c", t=TILES)
         input_features = invariant_input.rearrange("(p t) k -> p t k", t=TILES)
@@ -113,7 +111,11 @@ def tile_ryeelman_pa_kernel(
         def load_eq(q):
             rows = slice(LOAD_TILES * COMPONENTS * q, LOAD_TILES * COMPONENTS * (q + 1))
             nc.sync.dma_start(out=eq_sb[:, rows, FILL:CHANNELS], in_=hidden_vectors[:, rows, FILL - 1 :])
-            nc.sync.dma_start(out=eq_sb[:, rows, 1:FILL], in_=hidden_vectors[:, rows, 0 : FILL - 1])
+            nc.sync.dma_start(out=first_hidden[:, rows, 0 : FILL - 1], in_=hidden_vectors[:, rows, 0 : FILL - 1])
+
+        def place_first_hidden(q):
+            rows = slice(LOAD_TILES * COMPONENTS * q, LOAD_TILES * COMPONENTS * (q + 1))
+            nc.vector.tensor_copy(out=eq_sb[:, rows, 1:FILL], in_=first_hidden[:, rows, 0 : FILL - 1])
 
         def load_inv(q):
             tiles = slice(LOAD_TILES * q, LOAD_TILES * (q + 1))
@@ -325,6 +327,8 @@ def tile_ryeelman_pa_kernel(
         for step in range(-COMPONENTS * SQUARE_AHEAD, STEPS + COMPONENTS * TOTAL_BEHIND + FINISH_LAG + 1):
             t, j = divmod(step, COMPONENTS)
             later_t, later_j = divmod(step + LEFT_AHEAD, COMPONENTS)
+            if exists(t + SQUARE_AHEAD) and j == 0 and (t + SQUARE_AHEAD) % LOAD_TILES == 0:
+                place_first_hidden((t + SQUARE_AHEAD) // LOAD_TILES)
             if exists(later_t):
                 lefts(later_t, later_j)
             if exists(t):

@@ -28,22 +28,13 @@ N_TILE = 512
 HALVES = HIDDEN // N_TILE
 EPSILON = 1e-6
 FILL = 16
-LOAD_TILES = 2
-FLOW_BUFS = 4
-COPY_BUFS = 6
-TURN_BANKS = 3
-LEFT_BANKS = 2
-RIGHT_BANKS = 3
-
-SQUARE_AHEAD = 4
-RECIPROCAL_AHEAD = 3
-XN_AHEAD = 2
-LEFT_AHEAD = 1
-LINEAR_BEHIND = 1
-TOTAL_BEHIND = 2
+PAIR = 2
+BANKS = 8
+PREP_BUFS = 3
+COPY_BUFS = 8
+PRODUCT_BUFS = 6
+LAST_BUFS = 4
 STEPS = COMPONENTS * TILES
-FIRST_TANH = COMPONENTS * (TILES - 1 - RECIPROCAL_AHEAD) + 1
-FINISH_LAG = 2
 
 FLOPS = 2 * TOKENS * HIDDEN * (2 * COMPONENTS * CHANNELS + FEATURES)
 
@@ -67,11 +58,11 @@ def tile_ryeelman_pa_kernel(
     with ExitStack() as ctx:
         ctx.enter_context(tc.manual_schedule())
         keep = ctx.enter_context(tc.tile_pool(name="keep", bufs=1))
-        flow = ctx.enter_context(tc.tile_pool(name="flow", bufs=FLOW_BUFS))
+        prep = ctx.enter_context(tc.tile_pool(name="prep", bufs=PREP_BUFS))
         copies = ctx.enter_context(tc.tile_pool(name="copies", bufs=COPY_BUFS))
-        psum_turn = ctx.enter_context(tc.psum_pool(name="psum_turn", bufs=TURN_BANKS))
-        psum_left = ctx.enter_context(tc.psum_pool(name="psum_left", bufs=LEFT_BANKS))
-        psum_right = ctx.enter_context(tc.psum_pool(name="psum_right", bufs=RIGHT_BANKS))
+        products_pool = ctx.enter_context(tc.tile_pool(name="products", bufs=PRODUCT_BUFS))
+        last_pool = ctx.enter_context(tc.tile_pool(name="last", bufs=LAST_BUFS))
+        psum = ctx.enter_context(tc.psum_pool(name="psum", bufs=BANKS))
 
         identity = keep.tile([P, P], F32)
         first_channel = keep.tile([P, TILES * COMPONENTS], BF16)
@@ -86,10 +77,10 @@ def tile_ryeelman_pa_kernel(
         w_right = keep.tile([P, HIDDEN], U32, align_bytes=64)
         w_ii_planes = keep.tile([P, HIDDEN], U8, align_bytes=64)
         w_lr_planes = keep.tile([P, HIDDEN], U8, align_bytes=64)
-        inv_codes = keep.tile([P, INV_PASSES, TOKENS], U32, align_bytes=64)
-        inv_scales = keep.tile([P, INV_PASSES, TOKENS], U8, align_bytes=64)
-        xn_codes = keep.tile([P, COMPONENTS, TOKENS], U32, align_bytes=64)
-        xn_scales = keep.tile([P, COMPONENTS, TOKENS], U8, align_bytes=64)
+        wide_codes = keep.tile([P, TILES, 4, P], U32, align_bytes=64)
+        wide_scales = keep.tile([P, TILES, 4, P], U8, align_bytes=64)
+        narrow_codes = keep.tile([P, TILES, 2, P], U32, align_bytes=64)
+        narrow_scales = keep.tile([P, TILES, 2, P], U8, align_bytes=64)
         acc = [keep.tile([P, HIDDEN], F32, name="acc%d" % t) for t in range(TILES)]
 
         make_identity(nc, identity[:])
@@ -101,118 +92,87 @@ def tile_ryeelman_pa_kernel(
         nc.vector.memset(bias_row[:].bitcast(I32), 0)
         nc.vector.memset(ones[:], 1.0)
 
-        nc.sync.dma_start(out=first_channel[:], in_=equivariant_input.rearrange("(p t) j -> p (t j)", t=TILES))
-        nc.vector.tensor_copy(out=eq_sb[:, :, 0:1], in_=first_channel[:].unsqueeze(2))
-
         hidden_vectors = equivariant_hidden.rearrange("(p t) j c -> p (t j) c", t=TILES)
         input_features = invariant_input.rearrange("(p t) k -> p t k", t=TILES)
         hidden_features = invariant_hidden.rearrange("(p t) k -> p t k", t=TILES)
 
-        def load_eq(q):
-            rows = slice(LOAD_TILES * COMPONENTS * q, LOAD_TILES * COMPONENTS * (q + 1))
-            nc.sync.dma_start(out=eq_sb[:, rows, FILL:CHANNELS], in_=hidden_vectors[:, rows, FILL - 1 :])
+        def load_first_hidden(q):
+            rows = slice(PAIR * COMPONENTS * q, PAIR * COMPONENTS * (q + 1))
             nc.sync.dma_start(out=first_hidden[:, rows, 0 : FILL - 1], in_=hidden_vectors[:, rows, 0 : FILL - 1])
 
         def place_first_hidden(q):
-            rows = slice(LOAD_TILES * COMPONENTS * q, LOAD_TILES * COMPONENTS * (q + 1))
+            rows = slice(PAIR * COMPONENTS * q, PAIR * COMPONENTS * (q + 1))
             nc.vector.tensor_copy(out=eq_sb[:, rows, 1:FILL], in_=first_hidden[:, rows, 0 : FILL - 1])
 
-        def load_inv(q):
-            tiles = slice(LOAD_TILES * q, LOAD_TILES * (q + 1))
-            nc.sync.dma_start(out=inv_sb[:, tiles, 0:INPUT_FEATURES], in_=input_features[:, tiles, :])
-            nc.sync.dma_start(out=inv_sb[:, tiles, INPUT_FEATURES:FEATURES], in_=hidden_features[:, tiles, :])
+        def load_eq(t):
+            rows = slice(COMPONENTS * t, COMPONENTS * (t + 1))
+            nc.sync.dma_start(out=eq_sb[:, rows, FILL:CHANNELS], in_=hidden_vectors[:, rows, FILL - 1 :])
+
+        def load_inv(t):
+            nc.sync.dma_start(out=inv_sb[:, t, 0:INPUT_FEATURES], in_=input_features[:, t, :])
+            nc.sync.dma_start(out=inv_sb[:, t, INPUT_FEATURES:FEATURES], in_=hidden_features[:, t, :])
 
         def load_words(dst, words):
             nc.sync.dma_start(out=dst.bitcast(I32), in_=words.rearrange("p n t -> p (n t)").bitcast(I32))
 
-        def load_w_ii_scales():
-            for quadrant in range(4):
-                rows = slice(4 * quadrant, 4 * quadrant + 4)
-                nc.gpsimd.dma_start(
-                    out=w_ii_planes[32 * quadrant : 32 * quadrant + 4 * INV_PASSES, :].bitcast(F32),
-                    in_=W_ii_scales[:, rows, :].bitcast(F32),
-                )
+        for quadrant in range(4):
+            rows = slice(4 * quadrant, 4 * quadrant + 4)
+            nc.gpsimd.dma_start(
+                out=w_lr_planes[32 * quadrant : 32 * quadrant + 4, :].bitcast(F32),
+                in_=W_left_scales[0, rows, :].bitcast(F32),
+            )
+            nc.gpsimd.dma_start(
+                out=w_lr_planes[32 * quadrant + 4 : 32 * quadrant + 8, :].bitcast(F32),
+                in_=W_right_scales[0, rows, :].bitcast(F32),
+            )
+        for quadrant in range(4):
+            rows = slice(4 * quadrant, 4 * quadrant + 4)
+            nc.gpsimd.dma_start(
+                out=w_ii_planes[32 * quadrant : 32 * quadrant + 4 * INV_PASSES, :].bitcast(F32),
+                in_=W_ii_scales[:, rows, :].bitcast(F32),
+            )
 
-        def load_w_ii_words():
-            for g in range(INV_PASSES):
-                load_words(w_ii[:, g, :], W_ii_words[g])
-
-        def load_w_left_right_scales():
-            for quadrant in range(4):
-                rows = slice(4 * quadrant, 4 * quadrant + 4)
-                nc.gpsimd.dma_start(
-                    out=w_lr_planes[32 * quadrant : 32 * quadrant + 4, :].bitcast(F32),
-                    in_=W_left_scales[0, rows, :].bitcast(F32),
-                )
-                nc.gpsimd.dma_start(
-                    out=w_lr_planes[32 * quadrant + 4 : 32 * quadrant + 8, :].bitcast(F32),
-                    in_=W_right_scales[0, rows, :].bitcast(F32),
-                )
-
-        def load_w_left_right_words():
-            load_words(w_left[:], W_left_words[0])
-            load_words(w_right[:], W_right_words[0])
-
-        load_w_left_right_scales()
-        load_w_ii_scales()
+        nc.sync.dma_start(out=first_channel[:], in_=equivariant_input.rearrange("(p t) j -> p (t j)", t=TILES))
         nc.sync.dma_start(out=bias_row[0:1, :], in_=b_ii.rearrange("(o h) -> o h", o=1))
-        load_eq(0)
-        load_eq(1)
-        load_w_left_right_words()
-        load_inv(0)
-        load_w_ii_words()
-        load_eq(2)
-        load_inv(1)
-        load_eq(3)
-        load_inv(2)
-        load_inv(3)
+        for t in range(TILES):
+            if t % PAIR == 0:
+                load_first_hidden(t // PAIR)
+            load_eq(t)
+            load_inv(t)
+        load_words(w_left[:], W_left_words[0])
+        load_words(w_right[:], W_right_words[0])
+        for g in range(INV_PASSES):
+            load_words(w_ii[:, g, :], W_ii_words[g])
+
+        nc.vector.tensor_copy(out=eq_sb[:, :, 0:1], in_=first_channel[:].unsqueeze(2))
 
         for h in range(HALVES):
             cols = slice(h * N_TILE, (h + 1) * N_TILE)
-            spread = psum_right.tile([P, N_TILE], F32, tag="right")
+            spread = psum.tile([P, N_TILE], F32, tag="bank")
             nc.tensor.matmul(out=spread[:], lhsT=ones[:], rhs=bias_row[:, cols], start=True, stop=True)
-            nc.scalar.copy(out=bias_sb[:, cols], in_=spread[:])
+            nc.vector.tensor_copy(out=bias_sb[:, cols], in_=spread[:])
 
-        def transpose_words(words):
-            bank = psum_turn.tile([P, 2, P], F32, tag="turn")
+        def transpose_words(bank, slot, words):
             for u in range(2):
-                nc.tensor.transpose(bank[:, u, :], words[:, u:WORDS:2], identity[:])
-            return bank
-
-        turned_inv = {}
-
-        def turn_inv(t, g):
-            turned_inv[(t, g)] = transpose_words(inv_sb[:, t, g * K_PASS : (g + 1) * K_PASS].bitcast(F32))
-
-        def quantise_inv(t, g):
-            bank = turned_inv[(t, g)]
-            grouped = flow.tile([P, P, PACK], BF16, tag="inv_grouped", align_bytes=64)
-            nc.scalar.copy(
-                out=grouped[:].rearrange("p c t -> p (c t)").bitcast(F32).rearrange("p (c u) -> p c u", u=2),
-                in_=bank[:].rearrange("p u c -> p c u"),
-            )
-            nc.vector.quantize_mx(
-                out=inv_codes[:, g, t * P : (t + 1) * P].bitcast(FP8X4),
-                scales=inv_scales[:, g, t * P : (t + 1) * P],
-                in_=grouped[:].rearrange("p c t -> p (c t)"),
-            )
+                nc.tensor.transpose(bank[:, slot, u, :], words[:, u:WORDS:2], identity[:])
 
         squares = {}
         sums = {}
         recip = {}
-        grouped_xn = {}
+        turned = {}
+        wide = {}
+        narrow = {}
 
-        def square(t, j):
-            if j == 0:
-                squares[t] = flow.tile([P, COMPONENTS, CHANNELS], F32, name="squares")
+        def square(t):
+            squares[t] = prep.tile([P, COMPONENTS, CHANNELS], F32, name="squares")
             nc.scalar.activation(
-                out=squares[t][:, j, :].rearrange("p (r c) -> p r c", r=PACK),
-                in_=eq_sb[:, COMPONENTS * t + j, :].rearrange("p (c r) -> p r c", r=PACK),
+                out=squares[t][:].rearrange("p j (r c) -> p j r c", r=PACK),
+                in_=eq_sb[:, COMPONENTS * t : COMPONENTS * (t + 1), :].rearrange("p j (c r) -> p j r c", r=PACK),
                 func=ACT.Square,
             )
 
         def add_squares(t):
-            sums[t] = psum_turn.tile([P, PACK, P], F32, tag="turn", name="sums")
+            sums[t] = psum.tile([P, PACK, P], F32, tag="bank", name="sums")
             for r in range(PACK):
                 for j in range(COMPONENTS):
                     nc.tensor.matmul(
@@ -224,136 +184,167 @@ def tile_ryeelman_pa_kernel(
                         stop=(j == COMPONENTS - 1),
                     )
 
-        def reciprocal_sqrt(t):
-            recip[t] = flow.tile([P, CHANNELS], F32, name="recip")
+        def reciprocal(t):
+            recip[t] = prep.tile([P, CHANNELS], F32, name="recip")
             nc.scalar.activation(
                 out=recip[t][:],
                 in_=sums[t][:].rearrange("p r c -> p (r c)"),
                 func=ACT.Abs_reciprocal_sqrt,
                 bias=EPSILON,
             )
-
-        def reciprocal(t):
             nc.scalar.activation(out=recip[t][:], in_=recip[t][:], func=ACT.Square)
 
+        def turn(t):
+            banks = [psum.tile([P, 2, 2, P], F32, tag="bank", name="turned%d" % b) for b in range(3)]
+            pieces = [eq_sb[:, COMPONENTS * t + j, :] for j in range(COMPONENTS)]
+            pieces += [inv_sb[:, t, g * K_PASS : (g + 1) * K_PASS] for g in range(INV_PASSES)]
+            for i, piece in enumerate(pieces):
+                transpose_words(banks[i // 2], i % 2, piece.bitcast(F32))
+            turned[t] = banks
+
         def scale_xn(t, j):
-            bank = transpose_words(eq_sb[:, COMPONENTS * t + j, :].bitcast(F32))
-            grouped_xn[(t, j)] = flow.tile([P, P, 2, 2], BF16, name="grouped_xn", align_bytes=64)
+            if j == 0:
+                wide[t] = prep.tile([P, 4, P, 2, 2], BF16, name="wide", align_bytes=64)
+            bank = turned[t][j // 2]
             nc.vector.tensor_tensor(
-                out=grouped_xn[(t, j)][:],
-                in0=bank[:].rearrange("p u c -> p (u c)").bitcast(BF16).rearrange("p (u c e) -> p c u e", u=2, e=2),
+                out=wide[t][:, j, :, :, :],
+                in0=bank[:, j % 2, :, :]
+                .rearrange("p u c -> p (u c)")
+                .bitcast(BF16)
+                .rearrange("p (u c e) -> p c u e", u=2, e=2),
                 in1=recip[t][:].rearrange("p (u e c) -> p c u e", u=2, e=2),
                 op=ALU.mult,
             )
 
-        def quantise_xn(t, j):
+        def copy_first_inv(t):
+            nc.vector.tensor_copy(
+                out=wide[t][:, 3, :, :, :].rearrange("p c u e -> p (c u e)").bitcast(F32).rearrange("p (c u) -> p c u", u=2),
+                in_=turned[t][1][:, 1, :, :].rearrange("p u c -> p c u"),
+            )
+
+        def copy_other_inv(t):
+            narrow[t] = prep.tile([P, 2, P, PACK], BF16, name="narrow", align_bytes=64)
+            nc.scalar.copy(
+                out=narrow[t][:]
+                .rearrange("p g c k -> p (g c k)")
+                .bitcast(F32)
+                .rearrange("p (g c u) -> p g c u", g=2, u=2),
+                in_=turned[t][2][:].rearrange("p g u c -> p g c u"),
+            )
+
+        def quantise_narrow(t):
             nc.vector.quantize_mx(
-                out=xn_codes[:, j, t * P : (t + 1) * P].bitcast(FP8X4),
-                scales=xn_scales[:, j, t * P : (t + 1) * P],
-                in_=grouped_xn[(t, j)][:].rearrange("p c u e -> p (c u e)"),
+                out=narrow_codes[:, t, :, :].rearrange("p s c -> p (s c)").bitcast(FP8X4),
+                scales=narrow_scales[:, t, :, :].rearrange("p s c -> p (s c)"),
+                in_=narrow[t][:].rearrange("p g c k -> p (g c k)"),
             )
 
-        def linear_half(t, h):
-            tokens = slice(t * P, (t + 1) * P)
-            cols = slice(h * N_TILE, (h + 1) * N_TILE)
-            lin = psum_right.tile([P, N_TILE], F32, tag="right")
-            for g in range(INV_PASSES):
-                nc.tensor.matmul_mx(
-                    out=lin[:],
-                    lhsT=inv_codes[:, g, tokens].bitcast(FP8X4),
-                    lhsT_scale=inv_scales[:, g, tokens],
-                    rhs=w_ii[:, g, cols].bitcast(FP8X4),
-                    rhs_scale=w_ii_planes[4 * g : P, cols],
-                    start=(g == 0),
-                    stop=(g == INV_PASSES - 1),
-                )
-            nc.vector.tensor_tensor(out=last_product[t][:, cols], in0=lin[:], in1=last_product[t][:, cols], op=ALU.add)
-
-        def project(bank, t, j, h, words, first_row):
-            cols = slice(h * N_TILE, (h + 1) * N_TILE)
-            nc.tensor.matmul_mx(
-                out=bank[:],
-                lhsT=xn_codes[:, j, t * P : (t + 1) * P].bitcast(FP8X4),
-                lhsT_scale=xn_scales[:, j, t * P : (t + 1) * P],
-                rhs=words[:, cols].bitcast(FP8X4),
-                rhs_scale=w_lr_planes[first_row:P, cols],
-                start=True,
-                stop=True,
+        def quantise_wide(t):
+            nc.vector.quantize_mx(
+                out=wide_codes[:, t, :, :].rearrange("p s c -> p (s c)").bitcast(FP8X4),
+                scales=wide_scales[:, t, :, :].rearrange("p s c -> p (s c)"),
+                in_=wide[t][:].rearrange("p s c u e -> p (s c u e)"),
             )
-
-        last_product = {}
-
-        left_copies = {}
-
-        def lefts(t, j):
-            for h in range(HALVES):
-                left = psum_left.tile([P, N_TILE], F32, tag="left")
-                project(left, t, j, h, w_left, 0)
-                left_copies[(t, j, h)] = copies.tile([P, N_TILE], F32, name="left_sb")
-                nc.scalar.copy(out=left_copies[(t, j, h)][:], in_=left[:])
-
-        def products(t, j):
-            product = flow.tile([P, HIDDEN], F32, name="product", tag="product" if j < COMPONENTS - 1 else "last_product")
-            for h in range(HALVES):
-                right = psum_right.tile([P, N_TILE], F32, tag="right")
-                project(right, t, j, h, w_right, 4)
-                nc.vector.tensor_tensor(
-                    out=product[:, h * N_TILE : (h + 1) * N_TILE], in0=left_copies[(t, j, h)][:], in1=right[:], op=ALU.mult
-                )
-            if j == 0:
-                nc.gpsimd.tensor_tensor(out=acc[t][:], in0=product[:], in1=bias_sb[:], op=ALU.add)
-            elif j == 1:
-                nc.gpsimd.tensor_tensor(out=acc[t][:], in0=acc[t][:], in1=product[:], op=ALU.add)
-            else:
-                last_product[t] = product
-
-        def total(t):
-            for h in range(HALVES):
-                cols = slice(h * N_TILE, (h + 1) * N_TILE)
-                nc.vector.tensor_tensor(out=acc[t][:, cols], in0=acc[t][:, cols], in1=last_product[t][:, cols], op=ALU.add)
-
-        out_tiles = out.rearrange("(p t) h -> p t h", t=TILES)
-
-        def finish(t):
-            for h in range(HALVES):
-                cols = slice(h * N_TILE, (h + 1) * N_TILE)
-                nc.scalar.activation(out=acc[t][:, cols], in_=acc[t][:, cols], func=ACT.Tanh)
-                nc.sync.dma_start(out=out_tiles[:, t, cols], in_=acc[t][:, cols])
 
         def exists(t):
             return 0 <= t < TILES
 
-        finished = []
-        for step in range(-COMPONENTS * SQUARE_AHEAD, STEPS + COMPONENTS * TOTAL_BEHIND + FINISH_LAG + 1):
+        for i in range(-2, TILES):
+            if exists(i + 2) and (i + 2) % PAIR == 0:
+                place_first_hidden((i + 2) // PAIR)
+            if exists(i + 1):
+                add_squares(i + 1)
+            if exists(i):
+                turn(i)
+            if exists(i + 2):
+                square(i + 2)
+            if exists(i + 1):
+                reciprocal(i + 1)
+            if exists(i):
+                copy_other_inv(i)
+                scale_xn(i, 0)
+                scale_xn(i, 1)
+                copy_first_inv(i)
+                scale_xn(i, 2)
+                quantise_narrow(i)
+                quantise_wide(i)
+
+        nc.scalar.activation(out=warm[:], in_=warm[:], func=ACT.Tanh)
+
+        def multiply(bank, codes, scales, words, planes, first_row, h, start, stop):
+            cols = slice(h * N_TILE, (h + 1) * N_TILE)
+            nc.tensor.matmul_mx(
+                out=bank[:],
+                lhsT=codes.bitcast(FP8X4),
+                lhsT_scale=scales,
+                rhs=words[:, cols].bitcast(FP8X4),
+                rhs_scale=planes[first_row:P, cols],
+                start=start,
+                stop=stop,
+            )
+
+        def linear_half(t, h):
+            cols = slice(h * N_TILE, (h + 1) * N_TILE)
+            lin = psum.tile([P, N_TILE], F32, tag="bank", name="lin")
+            for g in range(INV_PASSES):
+                if g == 0:
+                    codes, scales = wide_codes[:, t, 3, :], wide_scales[:, t, 3, :]
+                else:
+                    codes, scales = narrow_codes[:, t, g - 1, :], narrow_scales[:, t, g - 1, :]
+                multiply(lin, codes, scales, w_ii[:, g, :], w_ii_planes, 4 * g, h, g == 0, g == INV_PASSES - 1)
+            nc.vector.tensor_tensor(out=acc[t][:, cols], in0=lin[:], in1=bias_sb[:, cols], op=ALU.add)
+
+        left_copies = {}
+        last_product = {}
+
+        def lefts(t, j):
+            for h in range(HALVES):
+                left = psum.tile([P, N_TILE], F32, tag="bank", name="left")
+                multiply(left, wide_codes[:, t, j, :], wide_scales[:, t, j, :], w_left, w_lr_planes, 0, h, True, True)
+                left_copies[(t, j, h)] = copies.tile([P, N_TILE], F32, name="left_sb")
+                nc.scalar.copy(out=left_copies[(t, j, h)][:], in_=left[:])
+
+        def products(t, j):
+            for h in range(HALVES):
+                cols = slice(h * N_TILE, (h + 1) * N_TILE)
+                right = psum.tile([P, N_TILE], F32, tag="bank", name="right")
+                multiply(right, wide_codes[:, t, j, :], wide_scales[:, t, j, :], w_right, w_lr_planes, 4, h, True, True)
+                if j < COMPONENTS - 1:
+                    product = products_pool.tile([P, N_TILE], F32, name="product")
+                else:
+                    product = last_pool.tile([P, N_TILE], F32, name="last_product")
+                    last_product[(t, h)] = product
+                nc.vector.tensor_tensor(out=product[:], in0=left_copies[(t, j, h)][:], in1=right[:], op=ALU.mult)
+                if j < COMPONENTS - 1:
+                    nc.gpsimd.tensor_tensor(out=acc[t][:, cols], in0=acc[t][:, cols], in1=product[:], op=ALU.add)
+
+        def total(t, h):
+            cols = slice(h * N_TILE, (h + 1) * N_TILE)
+            nc.vector.tensor_tensor(out=acc[t][:, cols], in0=acc[t][:, cols], in1=last_product[(t, h)][:], op=ALU.add)
+
+        out_tiles = out.rearrange("(p t) h -> p t h", t=TILES)
+
+        def finish(t, h):
+            cols = slice(h * N_TILE, (h + 1) * N_TILE)
+            nc.scalar.activation(out=acc[t][:, cols], in_=acc[t][:, cols], func=ACT.Tanh)
+            nc.sync.dma_start(out=out_tiles[:, t, cols], in_=acc[t][:, cols])
+
+        linear_half(0, 0)
+        linear_half(0, 1)
+        lefts(0, 0)
+        for step in range(STEPS):
             t, j = divmod(step, COMPONENTS)
-            later_t, later_j = divmod(step + LEFT_AHEAD, COMPONENTS)
-            if exists(t + SQUARE_AHEAD) and j == 0 and (t + SQUARE_AHEAD) % LOAD_TILES == 0:
-                place_first_hidden((t + SQUARE_AHEAD) // LOAD_TILES)
+            later_t, later_j = divmod(step + 1, COMPONENTS)
             if exists(later_t):
                 lefts(later_t, later_j)
-            if exists(t):
-                products(t, j)
-            if exists(t + XN_AHEAD):
-                scale_xn(t + XN_AHEAD, j)
-            if exists(t):
-                turn_inv(t, j)
-            if exists(t + SQUARE_AHEAD):
-                square(t + SQUARE_AHEAD, j)
-            if exists(t + RECIPROCAL_AHEAD) and j == 0:
-                add_squares(t + RECIPROCAL_AHEAD)
-            if exists(t - LINEAR_BEHIND) and j > 0:
-                linear_half(t - LINEAR_BEHIND, j - 1)
-            if exists(t - TOTAL_BEHIND) and j == 0:
-                total(t - TOTAL_BEHIND)
-            earlier_t, earlier_j = divmod(step - 1, COMPONENTS)
-            if exists(earlier_t + XN_AHEAD):
-                quantise_xn(earlier_t + XN_AHEAD, earlier_j)
-            if exists(t + RECIPROCAL_AHEAD) and j == 1:
-                reciprocal_sqrt(t + RECIPROCAL_AHEAD)
-            if exists(t + RECIPROCAL_AHEAD) and j == 2:
-                reciprocal(t + RECIPROCAL_AHEAD)
-            if exists(t):
-                quantise_inv(t, j)
-            if step >= FIRST_TANH and len(finished) < TILES and step >= COMPONENTS * (len(finished) + TOTAL_BEHIND) + FINISH_LAG:
-                finish(len(finished))
-                finished.append(step)
+            products(t, j)
+            if j < HALVES and exists(t + 1):
+                linear_half(t + 1, j)
+            if j < HALVES and exists(t - 1):
+                total(t - 1, j)
+            if j > 0 and exists(t - 1):
+                finish(t - 1, j - 1)
+        for h in range(HALVES):
+            total(TILES - 1, h)
+        for h in range(HALVES):
+            finish(TILES - 1, h)

@@ -30,7 +30,17 @@ EPSILON = 1e-6
 FILL = 16
 PAIR = 2
 BANKS = 8
+SUM_BANKS = (0, 1)
+EQ_BANKS = (2, 3, 4)
+INV_BANKS = (5, 6, 7)
+FIRST_PRODUCT_BANK = 7
+PIECES = COMPONENTS * TILES
+BANK_PIECES = 2
+CALL_PIECES = 4
+TURN_BANKS = PIECES // BANK_PIECES
+VECTOR_INV_BANKS = 3
 PREP_BUFS = 3
+SQUARE_BUFS = 2
 COPY_BUFS = 8
 PRODUCT_BUFS = 6
 LAST_BUFS = 4
@@ -59,10 +69,14 @@ def tile_ryeelman_pa_kernel(
         ctx.enter_context(tc.manual_schedule())
         keep = ctx.enter_context(tc.tile_pool(name="keep", bufs=1))
         prep = ctx.enter_context(tc.tile_pool(name="prep", bufs=PREP_BUFS))
+        square_pool = ctx.enter_context(tc.tile_pool(name="square_pool", bufs=SQUARE_BUFS))
         copies = ctx.enter_context(tc.tile_pool(name="copies", bufs=COPY_BUFS))
         products_pool = ctx.enter_context(tc.tile_pool(name="products", bufs=PRODUCT_BUFS))
         last_pool = ctx.enter_context(tc.tile_pool(name="last", bufs=LAST_BUFS))
-        psum = ctx.enter_context(tc.psum_pool(name="psum", bufs=BANKS))
+        psum = ctx.enter_context(tc.psum_pool(name="psum", bufs=1))
+
+        def bank_tile(b, shape, name):
+            return psum.tile(shape, F32, tag="bank%d" % b, name=name)
 
         identity = keep.tile([P, P], F32)
         first_channel = keep.tile([P, TILES * COMPONENTS], BF16)
@@ -77,10 +91,11 @@ def tile_ryeelman_pa_kernel(
         w_right = keep.tile([P, HIDDEN], U32, align_bytes=64)
         w_ii_planes = keep.tile([P, HIDDEN], U8, align_bytes=64)
         w_lr_planes = keep.tile([P, HIDDEN], U8, align_bytes=64)
-        wide_codes = keep.tile([P, TILES, 4, P], U32, align_bytes=64)
-        wide_scales = keep.tile([P, TILES, 4, P], U8, align_bytes=64)
-        narrow_codes = keep.tile([P, TILES, 2, P], U32, align_bytes=64)
-        narrow_scales = keep.tile([P, TILES, 2, P], U8, align_bytes=64)
+        xn_codes = keep.tile([P, PIECES, P], U32, align_bytes=64)
+        xn_scales = keep.tile([P, PIECES, P], U8, align_bytes=64)
+        inv_codes = keep.tile([P, PIECES, P], U32, align_bytes=64)
+        inv_scales = keep.tile([P, PIECES, P], U8, align_bytes=64)
+        recip = keep.tile([P, TILES, CHANNELS], F32)
         acc = [keep.tile([P, HIDDEN], F32, name="acc%d" % t) for t in range(TILES)]
 
         make_identity(nc, identity[:])
@@ -133,12 +148,18 @@ def tile_ryeelman_pa_kernel(
             )
 
         nc.sync.dma_start(out=first_channel[:], in_=equivariant_input.rearrange("(p t) j -> p (t j)", t=TILES))
-        nc.sync.dma_start(out=bias_row[0:1, :], in_=b_ii.rearrange("(o h) -> o h", o=1))
-        for t in range(TILES):
-            if t % PAIR == 0:
-                load_first_hidden(t // PAIR)
-            load_eq(t)
+        load_first_hidden(0)
+        load_eq(0)
+        load_first_hidden(1)
+        load_inv(0)
+        load_inv(1)
+        load_eq(1)
+        for q in range(2, TILES // PAIR):
+            load_first_hidden(q)
+        for t in range(2, TILES):
             load_inv(t)
+            load_eq(t)
+        nc.sync.dma_start(out=bias_row[0:1, :], in_=b_ii.rearrange("(o h) -> o h", o=1))
         load_words(w_left[:], W_left_words[0])
         load_words(w_right[:], W_right_words[0])
         for g in range(INV_PASSES):
@@ -146,25 +167,19 @@ def tile_ryeelman_pa_kernel(
 
         nc.vector.tensor_copy(out=eq_sb[:, :, 0:1], in_=first_channel[:].unsqueeze(2))
 
-        for h in range(HALVES):
-            cols = slice(h * N_TILE, (h + 1) * N_TILE)
-            spread = psum.tile([P, N_TILE], F32, tag="bank")
-            nc.tensor.matmul(out=spread[:], lhsT=ones[:], rhs=bias_row[:, cols], start=True, stop=True)
-            nc.vector.tensor_copy(out=bias_sb[:, cols], in_=spread[:])
-
         def transpose_words(bank, slot, words):
             for u in range(2):
                 nc.tensor.transpose(bank[:, slot, u, :], words[:, u:WORDS:2], identity[:])
 
         squares = {}
         sums = {}
-        recip = {}
-        turned = {}
-        wide = {}
-        narrow = {}
+        turned_eq = {}
+        turned_inv = {}
+        grouped_xn = {}
+        grouped_inv = {}
 
         def square(t):
-            squares[t] = prep.tile([P, COMPONENTS, CHANNELS], F32, name="squares")
+            squares[t] = square_pool.tile([P, COMPONENTS, CHANNELS], F32, name="squares")
             nc.scalar.activation(
                 out=squares[t][:].rearrange("p j (r c) -> p j r c", r=PACK),
                 in_=eq_sb[:, COMPONENTS * t : COMPONENTS * (t + 1), :].rearrange("p j (c r) -> p j r c", r=PACK),
@@ -172,7 +187,7 @@ def tile_ryeelman_pa_kernel(
             )
 
         def add_squares(t):
-            sums[t] = psum.tile([P, PACK, P], F32, tag="bank", name="sums")
+            sums[t] = bank_tile(SUM_BANKS[t % len(SUM_BANKS)], [P, PACK, P], "sums")
             for r in range(PACK):
                 for j in range(COMPONENTS):
                     nc.tensor.matmul(
@@ -185,91 +200,129 @@ def tile_ryeelman_pa_kernel(
                     )
 
         def reciprocal(t):
-            recip[t] = prep.tile([P, CHANNELS], F32, name="recip")
             nc.scalar.activation(
-                out=recip[t][:],
-                in_=sums[t][:].rearrange("p r c -> p (r c)"),
+                out=recip[:, t, :].rearrange("p (c r) -> p c r", r=PACK),
+                in_=sums[t][:].rearrange("p r c -> p c r"),
                 func=ACT.Abs_reciprocal_sqrt,
                 bias=EPSILON,
             )
-            nc.scalar.activation(out=recip[t][:], in_=recip[t][:], func=ACT.Square)
+            nc.scalar.activation(out=recip[:, t, :], in_=recip[:, t, :], func=ACT.Square)
 
-        def turn(t):
-            banks = [psum.tile([P, 2, 2, P], F32, tag="bank", name="turned%d" % b) for b in range(3)]
-            pieces = [eq_sb[:, COMPONENTS * t + j, :] for j in range(COMPONENTS)]
-            pieces += [inv_sb[:, t, g * K_PASS : (g + 1) * K_PASS] for g in range(INV_PASSES)]
-            for i, piece in enumerate(pieces):
-                transpose_words(banks[i // 2], i % 2, piece.bitcast(F32))
-            turned[t] = banks
+        def turn_eq(b):
+            turned_eq[b] = bank_tile(EQ_BANKS[b % len(EQ_BANKS)], [P, BANK_PIECES, 2, P], "turned_eq")
+            for s in range(BANK_PIECES):
+                transpose_words(turned_eq[b], s, eq_sb[:, BANK_PIECES * b + s, :].bitcast(F32))
 
-        def scale_xn(t, j):
-            if j == 0:
-                wide[t] = prep.tile([P, 4, P, 2, 2], BF16, name="wide", align_bytes=64)
-            bank = turned[t][j // 2]
-            nc.vector.tensor_tensor(
-                out=wide[t][:, j, :, :, :],
-                in0=bank[:, j % 2, :, :]
-                .rearrange("p u c -> p (u c)")
-                .bitcast(BF16)
-                .rearrange("p (u c e) -> p c u e", u=2, e=2),
-                in1=recip[t][:].rearrange("p (u e c) -> p c u e", u=2, e=2),
-                op=ALU.mult,
-            )
+        def turn_inv(b):
+            turned_inv[b] = bank_tile(INV_BANKS[b % len(INV_BANKS)], [P, BANK_PIECES, 2, P], "turned_inv")
+            for s in range(BANK_PIECES):
+                t, g = divmod(BANK_PIECES * b + s, INV_PASSES)
+                transpose_words(turned_inv[b], s, inv_sb[:, t, g * K_PASS : (g + 1) * K_PASS].bitcast(F32))
 
-        def copy_first_inv(t):
-            nc.vector.tensor_copy(
-                out=wide[t][:, 3, :, :, :].rearrange("p c u e -> p (c u e)").bitcast(F32).rearrange("p (c u) -> p c u", u=2),
-                in_=turned[t][1][:, 1, :, :].rearrange("p u c -> p c u"),
-            )
+        def scale_xn(b):
+            call, half = divmod(b, CALL_PIECES // BANK_PIECES)
+            if half == 0:
+                grouped_xn[call] = prep.tile([P, CALL_PIECES, P, 2, 2], BF16, name="grouped_xn", align_bytes=64)
+            for s in range(BANK_PIECES):
+                nc.vector.tensor_tensor(
+                    out=grouped_xn[call][:, BANK_PIECES * half + s, :, :, :],
+                    in0=turned_eq[b][:, s, :, :]
+                    .rearrange("p u c -> p (u c)")
+                    .bitcast(BF16)
+                    .rearrange("p (u c e) -> p c u e", u=2, e=2),
+                    in1=recip[:, (BANK_PIECES * b + s) // COMPONENTS, :].rearrange("p (c u e) -> p c u e", u=2, e=2),
+                    op=ALU.mult,
+                )
 
-        def copy_other_inv(t):
-            narrow[t] = prep.tile([P, 2, P, PACK], BF16, name="narrow", align_bytes=64)
-            nc.scalar.copy(
-                out=narrow[t][:]
-                .rearrange("p g c k -> p (g c k)")
+        def copy_inv(b):
+            call, half = divmod(b, CALL_PIECES // BANK_PIECES)
+            if half == 0:
+                grouped_inv[call] = prep.tile([P, CALL_PIECES, P, PACK], BF16, name="grouped_inv", align_bytes=64)
+            dst = (
+                grouped_inv[call][:, BANK_PIECES * half : BANK_PIECES * (half + 1), :, :]
+                .rearrange("p s c k -> p (s c k)")
                 .bitcast(F32)
-                .rearrange("p (g c u) -> p g c u", g=2, u=2),
-                in_=turned[t][2][:].rearrange("p g u c -> p g c u"),
+                .rearrange("p (s c u) -> p s c u", s=BANK_PIECES, u=2)
+            )
+            src = turned_inv[b][:].rearrange("p s u c -> p s c u")
+            if b < VECTOR_INV_BANKS:
+                nc.vector.tensor_copy(out=dst, in_=src)
+            else:
+                nc.scalar.copy(out=dst, in_=src)
+
+        def quantise(codes, scales, grouped, call):
+            pieces = slice(CALL_PIECES * call, CALL_PIECES * (call + 1))
+            nc.vector.quantize_mx(
+                out=codes[:, pieces, :].rearrange("p s c -> p (s c)").bitcast(FP8X4),
+                scales=scales[:, pieces, :].rearrange("p s c -> p (s c)"),
+                in_=grouped,
             )
 
-        def quantise_narrow(t):
-            nc.vector.quantize_mx(
-                out=narrow_codes[:, t, :, :].rearrange("p s c -> p (s c)").bitcast(FP8X4),
-                scales=narrow_scales[:, t, :, :].rearrange("p s c -> p (s c)"),
-                in_=narrow[t][:].rearrange("p g c k -> p (g c k)"),
-            )
+        def quantise_xn(call):
+            quantise(xn_codes, xn_scales, grouped_xn[call][:].rearrange("p s c u e -> p (s c u e)"), call)
 
-        def quantise_wide(t):
-            nc.vector.quantize_mx(
-                out=wide_codes[:, t, :, :].rearrange("p s c -> p (s c)").bitcast(FP8X4),
-                scales=wide_scales[:, t, :, :].rearrange("p s c -> p (s c)"),
-                in_=wide[t][:].rearrange("p s c u e -> p (s c u e)"),
-            )
+        def quantise_inv(call):
+            quantise(inv_codes, inv_scales, grouped_inv[call][:].rearrange("p s c k -> p (s c k)"), call)
 
         def exists(t):
             return 0 <= t < TILES
 
-        for i in range(-2, TILES):
-            if exists(i + 2) and (i + 2) % PAIR == 0:
-                place_first_hidden((i + 2) // PAIR)
-            if exists(i + 1):
-                add_squares(i + 1)
-            if exists(i):
-                turn(i)
-            if exists(i + 2):
-                square(i + 2)
-            if exists(i + 1):
-                reciprocal(i + 1)
-            if exists(i):
-                copy_other_inv(i)
-                scale_xn(i, 0)
-                scale_xn(i, 1)
-                copy_first_inv(i)
-                scale_xn(i, 2)
-                quantise_narrow(i)
-                quantise_wide(i)
+        place_first_hidden(0)
+        place_first_hidden(1)
+        square(0)
+        turn_inv(0)
+        copy_inv(0)
+        turn_inv(1)
+        copy_inv(1)
+        add_squares(0)
+        square(1)
+        turn_eq(0)
+        turn_inv(2)
+        for q in range(2, TILES // PAIR):
+            place_first_hidden(q)
+        quantise_inv(0)
+        reciprocal(0)
+        copy_inv(2)
+        inv_done = 3
+        eq_done = 0
+        for t in range(TILES):
+            if exists(t + 1):
+                add_squares(t + 1)
+            if exists(t + 2):
+                square(t + 2)
+            eq_until = (COMPONENTS * (t + 1)) // BANK_PIECES
+            for b in range(max(eq_done, 1), eq_until):
+                turn_eq(b)
+            inv_until = min(TURN_BANKS, inv_done + 2 - t % 2)
+            for b in range(inv_done, inv_until):
+                turn_inv(b)
+            if exists(t + 1):
+                reciprocal(t + 1)
+            for b in range(eq_done, eq_until):
+                scale_xn(b)
+                if b % 2 == 0 and b > 0:
+                    quantise_xn(b // 2 - 1)
+            for b in range(inv_done, inv_until):
+                copy_inv(b)
+            for b in range(inv_done, inv_until):
+                if b % 2 == 1:
+                    quantise_inv(b // 2)
+            eq_done = eq_until
+            inv_done = inv_until
+        quantise_xn(TURN_BANKS // 2 - 1)
 
+        for h in range(HALVES):
+            cols = slice(h * N_TILE, (h + 1) * N_TILE)
+            spread = bank_tile(INV_BANKS[h], [P, N_TILE], "spread")
+            nc.tensor.matmul(out=spread[:], lhsT=ones[:], rhs=bias_row[:, cols], start=True, stop=True)
+            nc.scalar.copy(out=bias_sb[:, cols], in_=spread[:])
         nc.scalar.activation(out=warm[:], in_=warm[:], func=ACT.Tanh)
+
+        banks_used = []
+
+        def next_bank(name):
+            banks_used.append(name)
+            return bank_tile((FIRST_PRODUCT_BANK + len(banks_used) - 1) % BANKS, [P, N_TILE], name)
 
         def multiply(bank, codes, scales, words, planes, first_row, h, start, stop):
             cols = slice(h * N_TILE, (h + 1) * N_TILE)
@@ -285,13 +338,13 @@ def tile_ryeelman_pa_kernel(
 
         def linear_half(t, h):
             cols = slice(h * N_TILE, (h + 1) * N_TILE)
-            lin = psum.tile([P, N_TILE], F32, tag="bank", name="lin")
+            lin = next_bank("lin")
             for g in range(INV_PASSES):
-                if g == 0:
-                    codes, scales = wide_codes[:, t, 3, :], wide_scales[:, t, 3, :]
-                else:
-                    codes, scales = narrow_codes[:, t, g - 1, :], narrow_scales[:, t, g - 1, :]
-                multiply(lin, codes, scales, w_ii[:, g, :], w_ii_planes, 4 * g, h, g == 0, g == INV_PASSES - 1)
+                piece = INV_PASSES * t + g
+                multiply(
+                    lin, inv_codes[:, piece, :], inv_scales[:, piece, :], w_ii[:, g, :], w_ii_planes, 4 * g, h,
+                    g == 0, g == INV_PASSES - 1,
+                )
             nc.vector.tensor_tensor(out=acc[t][:, cols], in0=lin[:], in1=bias_sb[:, cols], op=ALU.add)
 
         left_copies = {}
@@ -299,16 +352,18 @@ def tile_ryeelman_pa_kernel(
 
         def lefts(t, j):
             for h in range(HALVES):
-                left = psum.tile([P, N_TILE], F32, tag="bank", name="left")
-                multiply(left, wide_codes[:, t, j, :], wide_scales[:, t, j, :], w_left, w_lr_planes, 0, h, True, True)
+                left = next_bank("left")
+                piece = COMPONENTS * t + j
+                multiply(left, xn_codes[:, piece, :], xn_scales[:, piece, :], w_left, w_lr_planes, 0, h, True, True)
                 left_copies[(t, j, h)] = copies.tile([P, N_TILE], F32, name="left_sb")
                 nc.scalar.copy(out=left_copies[(t, j, h)][:], in_=left[:])
 
         def products(t, j):
             for h in range(HALVES):
                 cols = slice(h * N_TILE, (h + 1) * N_TILE)
-                right = psum.tile([P, N_TILE], F32, tag="bank", name="right")
-                multiply(right, wide_codes[:, t, j, :], wide_scales[:, t, j, :], w_right, w_lr_planes, 4, h, True, True)
+                right = next_bank("right")
+                piece = COMPONENTS * t + j
+                multiply(right, xn_codes[:, piece, :], xn_scales[:, piece, :], w_right, w_lr_planes, 4, h, True, True)
                 if j < COMPONENTS - 1:
                     product = products_pool.tile([P, N_TILE], F32, name="product")
                 else:

@@ -42,8 +42,9 @@ VECTOR_INV_BANKS = 3
 PREP_BUFS = 3
 SQUARE_BUFS = 2
 COPY_BUFS = 8
-PRODUCT_BUFS = 6
-LAST_BUFS = 4
+PRODUCT_BUFS = 8
+GPSIMD_ADDS = ((0, 0), (0, 1), (1, 0))
+VECTOR_ADDS = ((1, 1), (2, 0), (2, 1))
 STEPS = COMPONENTS * TILES
 
 FLOPS = 2 * TOKENS * HIDDEN * (2 * COMPONENTS * CHANNELS + FEATURES)
@@ -72,7 +73,6 @@ def tile_ryeelman_pa_kernel(
         square_pool = ctx.enter_context(tc.tile_pool(name="square_pool", bufs=SQUARE_BUFS))
         copies = ctx.enter_context(tc.tile_pool(name="copies", bufs=COPY_BUFS))
         products_pool = ctx.enter_context(tc.tile_pool(name="products", bufs=PRODUCT_BUFS))
-        last_pool = ctx.enter_context(tc.tile_pool(name="last", bufs=LAST_BUFS))
         psum = ctx.enter_context(tc.psum_pool(name="psum", bufs=1))
 
         def bank_tile(b, shape, name):
@@ -348,7 +348,7 @@ def tile_ryeelman_pa_kernel(
             nc.vector.tensor_tensor(out=acc[t][:, cols], in0=lin[:], in1=bias_sb[:, cols], op=ALU.add)
 
         left_copies = {}
-        last_product = {}
+        product_tiles = {}
 
         def lefts(t, j):
             for h in range(HALVES):
@@ -358,24 +358,21 @@ def tile_ryeelman_pa_kernel(
                 left_copies[(t, j, h)] = copies.tile([P, N_TILE], F32, name="left_sb")
                 nc.scalar.copy(out=left_copies[(t, j, h)][:], in_=left[:])
 
+        def add_product(engine, t, j, h):
+            cols = slice(h * N_TILE, (h + 1) * N_TILE)
+            engine.tensor_tensor(out=acc[t][:, cols], in0=acc[t][:, cols], in1=product_tiles[(t, j, h)][:], op=ALU.add)
+
         def products(t, j):
             for h in range(HALVES):
-                cols = slice(h * N_TILE, (h + 1) * N_TILE)
                 right = next_bank("right")
                 piece = COMPONENTS * t + j
                 multiply(right, xn_codes[:, piece, :], xn_scales[:, piece, :], w_right, w_lr_planes, 4, h, True, True)
-                if j < COMPONENTS - 1:
-                    product = products_pool.tile([P, N_TILE], F32, name="product")
-                else:
-                    product = last_pool.tile([P, N_TILE], F32, name="last_product")
-                    last_product[(t, h)] = product
-                nc.vector.tensor_tensor(out=product[:], in0=left_copies[(t, j, h)][:], in1=right[:], op=ALU.mult)
-                if j < COMPONENTS - 1:
-                    nc.gpsimd.tensor_tensor(out=acc[t][:, cols], in0=acc[t][:, cols], in1=product[:], op=ALU.add)
-
-        def total(t, h):
-            cols = slice(h * N_TILE, (h + 1) * N_TILE)
-            nc.vector.tensor_tensor(out=acc[t][:, cols], in0=acc[t][:, cols], in1=last_product[(t, h)][:], op=ALU.add)
+                product_tiles[(t, j, h)] = products_pool.tile([P, N_TILE], F32, name="product")
+                nc.vector.tensor_tensor(
+                    out=product_tiles[(t, j, h)][:], in0=left_copies[(t, j, h)][:], in1=right[:], op=ALU.mult
+                )
+                if (j, h) in GPSIMD_ADDS:
+                    add_product(nc.gpsimd, t, j, h)
 
         out_tiles = out.rearrange("(p t) h -> p t h", t=TILES)
 
@@ -393,13 +390,13 @@ def tile_ryeelman_pa_kernel(
             if exists(later_t):
                 lefts(later_t, later_j)
             products(t, j)
-            if j < HALVES and exists(t + 1):
-                linear_half(t + 1, j)
+            if j == COMPONENTS - 1:
+                if exists(t + 1):
+                    linear_half(t + 1, 0)
+                    linear_half(t + 1, 1)
+                for add_j, add_h in VECTOR_ADDS:
+                    add_product(nc.vector, t, add_j, add_h)
             if j < HALVES and exists(t - 1):
-                total(t - 1, j)
-            if j > 0 and exists(t - 1):
-                finish(t - 1, j - 1)
-        for h in range(HALVES):
-            total(TILES - 1, h)
+                finish(t - 1, j)
         for h in range(HALVES):
             finish(TILES - 1, h)

@@ -33,12 +33,13 @@ BANKS = 8
 SUM_BANKS = (0, 1)
 EQ_BANKS = (2, 3, 4)
 INV_BANKS = (5, 6, 7)
-FIRST_PRODUCT_BANK = 7
+FIRST_PRODUCT_BANK = 2
 PIECES = COMPONENTS * TILES
 BANK_PIECES = 2
 CALL_PIECES = 4
 TURN_BANKS = PIECES // BANK_PIECES
-VECTOR_INV_BANKS = 3
+VECTOR_INV_BANKS = 6
+HEAD_INV_BANKS = 3
 PREP_BUFS = 3
 SQUARE_BUFS = 2
 COPY_BUFS = 8
@@ -156,10 +157,14 @@ def tile_ryeelman_pa_kernel(
         load_eq(1)
         for q in range(2, TILES // PAIR):
             load_first_hidden(q)
-        for t in range(2, TILES):
-            load_inv(t)
+        for t in range(2, TILES // 2):
             load_eq(t)
+            load_inv(t)
         nc.sync.dma_start(out=bias_row[0:1, :], in_=b_ii.rearrange("(o h) -> o h", o=1))
+        for t in range(TILES // 2, TILES):
+            load_eq(t)
+        for t in range(TILES // 2, TILES):
+            load_inv(t)
         load_words(w_left[:], W_left_words[0])
         load_words(w_right[:], W_right_words[0])
         for g in range(INV_PASSES):
@@ -283,40 +288,47 @@ def tile_ryeelman_pa_kernel(
         quantise_inv(0)
         reciprocal(0)
         copy_inv(2)
-        inv_done = 3
-        eq_done = 0
-        for t in range(TILES):
+        add_squares(1)
+        square(2)
+        scale_xn(0)
+        for b in range(HEAD_INV_BANKS, VECTOR_INV_BANKS):
+            turn_inv(b)
+            copy_inv(b)
+            if b == HEAD_INV_BANKS + 1:
+                quantise_inv(1)
+        eq_done = 1
+        for t in range(1, TILES):
             if exists(t + 1):
                 add_squares(t + 1)
             if exists(t + 2):
                 square(t + 2)
             eq_until = (COMPONENTS * (t + 1)) // BANK_PIECES
-            for b in range(max(eq_done, 1), eq_until):
+            for b in range(eq_done, eq_until):
                 turn_eq(b)
-            inv_until = min(TURN_BANKS, inv_done + 2 - t % 2)
-            for b in range(inv_done, inv_until):
-                turn_inv(b)
-            if exists(t + 1):
-                reciprocal(t + 1)
+            if TILES - 1 - len(INV_BANKS) <= t < TILES - 1:
+                turn_inv(VECTOR_INV_BANKS + t - (TILES - 1 - len(INV_BANKS)))
+            reciprocal(t)
             for b in range(eq_done, eq_until):
                 scale_xn(b)
-                if b % 2 == 0 and b > 0:
+                if b % 2 == 0:
                     quantise_xn(b // 2 - 1)
-            for b in range(inv_done, inv_until):
-                copy_inv(b)
-            for b in range(inv_done, inv_until):
-                if b % 2 == 1:
-                    quantise_inv(b // 2)
+            if t == 1:
+                quantise_inv(2)
             eq_done = eq_until
-            inv_done = inv_until
-        quantise_xn(TURN_BANKS // 2 - 1)
-
+        spread = [bank_tile(SUM_BANKS[h], [P, N_TILE], "spread%d" % h) for h in range(HALVES)]
         for h in range(HALVES):
-            cols = slice(h * N_TILE, (h + 1) * N_TILE)
-            spread = bank_tile(INV_BANKS[h], [P, N_TILE], "spread")
-            nc.tensor.matmul(out=spread[:], lhsT=ones[:], rhs=bias_row[:, cols], start=True, stop=True)
-            nc.scalar.copy(out=bias_sb[:, cols], in_=spread[:])
-        nc.scalar.activation(out=warm[:], in_=warm[:], func=ACT.Tanh)
+            nc.tensor.matmul(
+                out=spread[h][:], lhsT=ones[:], rhs=bias_row[:, h * N_TILE : (h + 1) * N_TILE], start=True, stop=True
+            )
+        for b in range(VECTOR_INV_BANKS, TURN_BANKS):
+            if b >= VECTOR_INV_BANKS + len(INV_BANKS):
+                turn_inv(b)
+            copy_inv(b)
+        for h in range(HALVES):
+            nc.scalar.copy(out=bias_sb[:, h * N_TILE : (h + 1) * N_TILE], in_=spread[h][:])
+        quantise_xn(TURN_BANKS // 2 - 1)
+        for call in range(VECTOR_INV_BANKS // 2, TURN_BANKS // 2):
+            quantise_inv(call)
 
         banks_used = []
 
@@ -381,14 +393,16 @@ def tile_ryeelman_pa_kernel(
             nc.scalar.activation(out=acc[t][:, cols], in_=acc[t][:, cols], func=ACT.Tanh)
             nc.sync.dma_start(out=out_tiles[:, t, cols], in_=acc[t][:, cols])
 
+        lefts(0, 0)
         linear_half(0, 0)
         linear_half(0, 1)
-        lefts(0, 0)
         for step in range(STEPS):
             t, j = divmod(step, COMPONENTS)
             later_t, later_j = divmod(step + 1, COMPONENTS)
             if exists(later_t):
                 lefts(later_t, later_j)
+            if step == 1:
+                nc.scalar.activation(out=warm[:], in_=warm[:], func=ACT.Tanh)
             products(t, j)
             if j == COMPONENTS - 1:
                 if exists(t + 1):

@@ -131,23 +131,6 @@ def tile_ryeelman_pa_kernel(
         def load_words(dst, words):
             nc.sync.dma_start(out=dst.bitcast(I32), in_=words.rearrange("p n t -> p (n t)").bitcast(I32))
 
-        for quadrant in range(4):
-            rows = slice(4 * quadrant, 4 * quadrant + 4)
-            nc.gpsimd.dma_start(
-                out=w_lr_planes[32 * quadrant : 32 * quadrant + 4, :].bitcast(F32),
-                in_=W_left_scales[0, rows, :].bitcast(F32),
-            )
-            nc.gpsimd.dma_start(
-                out=w_lr_planes[32 * quadrant + 4 : 32 * quadrant + 8, :].bitcast(F32),
-                in_=W_right_scales[0, rows, :].bitcast(F32),
-            )
-        for quadrant in range(4):
-            rows = slice(4 * quadrant, 4 * quadrant + 4)
-            nc.gpsimd.dma_start(
-                out=w_ii_planes[32 * quadrant : 32 * quadrant + 4 * INV_PASSES, :].bitcast(F32),
-                in_=W_ii_scales[:, rows, :].bitcast(F32),
-            )
-
         nc.sync.dma_start(out=first_channel[:], in_=equivariant_input.rearrange("(p t) j -> p (t j)", t=TILES))
         load_first_hidden(0)
         load_eq(0)
@@ -169,6 +152,22 @@ def tile_ryeelman_pa_kernel(
         load_words(w_right[:], W_right_words[0])
         for g in range(INV_PASSES):
             load_words(w_ii[:, g, :], W_ii_words[g])
+        for quadrant in range(4):
+            rows = slice(4 * quadrant, 4 * quadrant + 4)
+            nc.sync.dma_start(
+                out=w_ii_planes[32 * quadrant : 32 * quadrant + 4 * INV_PASSES, :].bitcast(I32),
+                in_=W_ii_scales[:, rows, :].bitcast(I32),
+            )
+        for quadrant in range(4):
+            rows = slice(4 * quadrant, 4 * quadrant + 4)
+            nc.sync.dma_start(
+                out=w_lr_planes[32 * quadrant : 32 * quadrant + 4, :].bitcast(I32),
+                in_=W_left_scales[0, rows, :].bitcast(I32),
+            )
+            nc.sync.dma_start(
+                out=w_lr_planes[32 * quadrant + 4 : 32 * quadrant + 8, :].bitcast(I32),
+                in_=W_right_scales[0, rows, :].bitcast(I32),
+            )
 
         nc.vector.tensor_copy(out=eq_sb[:, :, 0:1], in_=first_channel[:].unsqueeze(2))
 

@@ -184,10 +184,15 @@ def tile_ryeelman_pa_kernel(
 
         def square(t):
             squares[t] = square_pool.tile([P, COMPONENTS, CHANNELS], F32, name="squares")
+            scalars = COMPONENTS - 1
             nc.scalar.activation(
-                out=squares[t][:].rearrange("p j (r c) -> p j r c", r=PACK),
-                in_=eq_sb[:, COMPONENTS * t : COMPONENTS * (t + 1), :].rearrange("p j (c r) -> p j r c", r=PACK),
+                out=squares[t][:, 0:scalars, :].rearrange("p j (r c) -> p j r c", r=PACK),
+                in_=eq_sb[:, COMPONENTS * t : COMPONENTS * t + scalars, :].rearrange("p j (c r) -> p j r c", r=PACK),
                 func=ACT.Square,
+            )
+            third = eq_sb[:, COMPONENTS * t + scalars, :].rearrange("p (c r) -> p r c", r=PACK)
+            nc.gpsimd.tensor_tensor(
+                out=squares[t][:, scalars, :].rearrange("p (r c) -> p r c", r=PACK), in0=third, in1=third, op=ALU.mult
             )
 
         def add_squares(t):

@@ -191,9 +191,10 @@ def tile_ryeelman_pa_kernel(
                 func=ACT.Square,
             )
             third = eq_sb[:, COMPONENTS * t + scalars, :].rearrange("p (c r) -> p r c", r=PACK)
-            nc.gpsimd.tensor_tensor(
-                out=squares[t][:, scalars, :].rearrange("p (r c) -> p r c", r=PACK), in0=third, in1=third, op=ALU.mult
-            )
+            for r in range(PACK):
+                nc.gpsimd.tensor_tensor(
+                    out=squares[t][:, scalars, r * P : (r + 1) * P], in0=third[:, r, :], in1=third[:, r, :], op=ALU.mult
+                )
 
         def add_squares(t):
             sums[t] = bank_tile(SUM_BANKS[t % len(SUM_BANKS)], [P, PACK, P], "sums")

@@ -35,6 +35,7 @@ EQ_BANKS = (2, 3, 4)
 INV_BANKS = (5, 6, 7)
 FIRST_PRODUCT_BANK = 2
 PIECES = COMPONENTS * TILES
+PAIR_TILES = 2
 BANK_PIECES = 2
 CALL_PIECES = 4
 TURN_BANKS = PIECES // BANK_PIECES
@@ -46,7 +47,9 @@ COPY_BUFS = 8
 PRODUCT_BUFS = 8
 GPSIMD_ADDS = ((0, 0), (0, 1), (1, 0))
 VECTOR_ADDS = ((1, 1), (2, 0), (2, 1))
-STEPS = COMPONENTS * TILES
+BLOCKS = HIDDEN // P
+UNIT_BLOCKS = 2
+PAIR_TOKENS = PAIR * P
 
 FLOPS = 2 * TOKENS * HIDDEN * (2 * COMPONENTS * CHANNELS + FEATURES)
 
@@ -74,6 +77,7 @@ def tile_ryeelman_pa_kernel(
         square_pool = ctx.enter_context(tc.tile_pool(name="square_pool", bufs=SQUARE_BUFS))
         copies = ctx.enter_context(tc.tile_pool(name="copies", bufs=COPY_BUFS))
         products_pool = ctx.enter_context(tc.tile_pool(name="products", bufs=PRODUCT_BUFS))
+        results = ctx.enter_context(tc.tile_pool(name="results", bufs=6))
         psum = ctx.enter_context(tc.psum_pool(name="psum", bufs=1))
 
         def bank_tile(b, shape, name):
@@ -97,7 +101,10 @@ def tile_ryeelman_pa_kernel(
         inv_codes = keep.tile([P, PIECES, P], U32, align_bytes=64)
         inv_scales = keep.tile([P, PIECES, P], U8, align_bytes=64)
         recip = keep.tile([P, TILES, CHANNELS], F32)
-        acc = [keep.tile([P, HIDDEN], F32, name="acc%d" % t) for t in range(TILES)]
+        acc = {}
+        bias_rows = keep.tile([P, P], BF16)
+        bias_words = keep.tile([P, P], F32)
+        bias_cols = keep.tile([P, BLOCKS], F32)
 
         make_identity(nc, identity[:])
         warm = keep.tile([P, 1], F32)
@@ -106,6 +113,7 @@ def tile_ryeelman_pa_kernel(
         nc.vector.memset(w_ii_planes[:].bitcast(I32), 0)
         nc.vector.memset(w_lr_planes[:].bitcast(I32), 0)
         nc.vector.memset(bias_row[:].bitcast(I32), 0)
+        nc.vector.memset(bias_rows[:].bitcast(I32), 0)
         nc.vector.memset(ones[:], 1.0)
 
         hidden_vectors = equivariant_hidden.rearrange("(p t) j c -> p (t j) c", t=TILES)
@@ -135,8 +143,10 @@ def tile_ryeelman_pa_kernel(
         load_first_hidden(0)
         load_eq(0)
         load_first_hidden(1)
-        load_inv(0)
-        load_inv(1)
+        for t in range(PAIR_TILES):
+            nc.sync.dma_start(out=inv_sb[:, t, 0:INPUT_FEATURES], in_=input_features[:, t, :])
+        for t in range(PAIR_TILES):
+            nc.sync.dma_start(out=inv_sb[:, t, INPUT_FEATURES:FEATURES], in_=hidden_features[:, t, :])
         load_eq(1)
         for q in range(2, TILES // PAIR):
             load_first_hidden(q)
@@ -144,6 +154,7 @@ def tile_ryeelman_pa_kernel(
             load_eq(t)
             load_inv(t)
         nc.sync.dma_start(out=bias_row[0:1, :], in_=b_ii.rearrange("(o h) -> o h", o=1))
+        nc.sync.dma_start(out=bias_rows[0:BLOCKS, :], in_=b_ii.rearrange("(r h) -> r h", r=BLOCKS))
         for t in range(TILES // 2, TILES):
             load_eq(t)
         for t in range(TILES // 2, TILES):
@@ -174,6 +185,17 @@ def tile_ryeelman_pa_kernel(
         def transpose_words(bank, slot, words):
             for u in range(2):
                 nc.tensor.transpose(bank[:, slot, u, :], words[:, u:WORDS:2], identity[:])
+
+        def piece_of(t, j):
+            if t < PAIR_TILES:
+                return PAIR * COMPONENTS * (t // PAIR) + PAIR * j + t % PAIR
+            return COMPONENTS * t + j
+
+        def part_of(piece):
+            if piece < COMPONENTS * PAIR_TILES:
+                q, rest = divmod(piece, PAIR * COMPONENTS)
+                return PAIR * q + rest % PAIR, rest // PAIR
+            return divmod(piece, COMPONENTS)
 
         squares = {}
         sums = {}
@@ -226,21 +248,22 @@ def tile_ryeelman_pa_kernel(
         def turn_inv(b):
             turned_inv[b] = bank_tile(INV_BANKS[b % len(INV_BANKS)], [P, BANK_PIECES, 2, P], "turned_inv")
             for s in range(BANK_PIECES):
-                t, g = divmod(BANK_PIECES * b + s, INV_PASSES)
+                t, g = part_of(BANK_PIECES * b + s)
                 transpose_words(turned_inv[b], s, inv_sb[:, t, g * K_PASS : (g + 1) * K_PASS].bitcast(F32))
 
         def scale_xn(b):
-            call, half = divmod(b, CALL_PIECES // BANK_PIECES)
-            if half == 0:
-                grouped_xn[call] = prep.tile([P, CALL_PIECES, P, 2, 2], BF16, name="grouped_xn", align_bytes=64)
             for s in range(BANK_PIECES):
+                t, j = divmod(BANK_PIECES * b + s, COMPONENTS)
+                call, place = divmod(piece_of(t, j), CALL_PIECES)
+                if call not in grouped_xn:
+                    grouped_xn[call] = prep.tile([P, CALL_PIECES, P, 2, 2], BF16, name="grouped_xn", align_bytes=64)
                 nc.vector.tensor_tensor(
-                    out=grouped_xn[call][:, BANK_PIECES * half + s, :, :, :],
+                    out=grouped_xn[call][:, place, :, :, :],
                     in0=turned_eq[b][:, s, :, :]
                     .rearrange("p u c -> p (u c)")
                     .bitcast(BF16)
                     .rearrange("p (u c e) -> p c u e", u=2, e=2),
-                    in1=recip[:, (BANK_PIECES * b + s) // COMPONENTS, :].rearrange("p (c u e) -> p c u e", u=2, e=2),
+                    in1=recip[:, t, :].rearrange("p (c u e) -> p c u e", u=2, e=2),
                     op=ALU.mult,
                 )
 
@@ -329,6 +352,7 @@ def tile_ryeelman_pa_kernel(
             if b >= VECTOR_INV_BANKS + len(INV_BANKS):
                 turn_inv(b)
             copy_inv(b)
+        nc.vector.tensor_copy(out=bias_words[:], in_=bias_rows[:])
         for h in range(HALVES):
             nc.scalar.copy(out=bias_sb[:, h * N_TILE : (h + 1) * N_TILE], in_=spread[h][:])
         quantise_xn(TURN_BANKS // 2 - 1)
@@ -353,69 +377,164 @@ def tile_ryeelman_pa_kernel(
                 stop=stop,
             )
 
-        def linear_half(t, h):
-            cols = slice(h * N_TILE, (h + 1) * N_TILE)
-            lin = next_bank("lin")
-            for g in range(INV_PASSES):
-                piece = INV_PASSES * t + g
-                multiply(
-                    lin, inv_codes[:, piece, :], inv_scales[:, piece, :], w_ii[:, g, :], w_ii_planes, 4 * g, h,
-                    g == 0, g == INV_PASSES - 1,
-                )
-            nc.vector.tensor_tensor(out=acc[t][:, cols], in0=lin[:], in1=bias_sb[:, cols], op=ALU.add)
+        def multiply_turned(bank, b, codes, scales, words, planes, first_row, start, stop):
+            cols = slice((b % UNIT_BLOCKS) * PAIR_TOKENS, (b % UNIT_BLOCKS + 1) * PAIR_TOKENS)
+            hidden = slice(b * P, (b + 1) * P)
+            nc.tensor.matmul_mx(
+                out=bank[:, cols],
+                lhsT=words[:, hidden].bitcast(FP8X4),
+                lhsT_scale=planes[first_row:P, hidden],
+                rhs=codes.rearrange("p s c -> p (s c)").bitcast(FP8X4),
+                rhs_scale=scales.rearrange("p s c -> p (s c)"),
+                start=start,
+                stop=stop,
+            )
+
+        def pair_pieces(q, j):
+            first = PAIR * COMPONENTS * q + PAIR * j
+            return slice(first, first + PAIR)
+
+        def unit_blocks(u):
+            return range(UNIT_BLOCKS * u, UNIT_BLOCKS * (u + 1))
+
+        def factor(job, words, planes, first_row, name):
+            kind, i, j, h = job
+            bank = next_bank(name)
+            if kind == "tile":
+                piece = piece_of(i, j)
+                multiply(bank, xn_codes[:, piece, :], xn_scales[:, piece, :], words, planes, first_row, h, True, True)
+            else:
+                pieces = pair_pieces(i, j)
+                for b in unit_blocks(h):
+                    multiply_turned(bank, b, xn_codes[:, pieces, :], xn_scales[:, pieces, :], words, planes, first_row, True, True)
+            return bank
 
         left_copies = {}
         product_tiles = {}
 
-        def lefts(t, j):
-            for h in range(HALVES):
-                left = next_bank("left")
-                piece = COMPONENTS * t + j
-                multiply(left, xn_codes[:, piece, :], xn_scales[:, piece, :], w_left, w_lr_planes, 0, h, True, True)
-                left_copies[(t, j, h)] = copies.tile([P, N_TILE], F32, name="left_sb")
-                nc.scalar.copy(out=left_copies[(t, j, h)][:], in_=left[:])
+        def left(job):
+            bank = factor(job, w_left, w_lr_planes, 0, "left")
+            left_copies[job] = copies.tile([P, N_TILE], F32, name="left_sb")
+            nc.scalar.copy(out=left_copies[job][:], in_=bank[:])
+
+        def right(job):
+            bank = factor(job, w_right, w_lr_planes, 4, "right")
+            product_tiles[job] = products_pool.tile([P, N_TILE], F32, name=job[0] + "_product", bufs=8 if job[0] == "tile" else 6)
+            nc.vector.tensor_tensor(out=product_tiles[job][:], in0=left_copies[job][:], in1=bank[:], op=ALU.mult)
+
+        acc = {}
+
+        def linear_half(t, h):
+            lin = next_bank("lin")
+            for g in range(INV_PASSES):
+                piece = piece_of(t, g)
+                multiply(
+                    lin, inv_codes[:, piece, :], inv_scales[:, piece, :], w_ii[:, g, :], w_ii_planes, 4 * g, h,
+                    g == 0, g == INV_PASSES - 1,
+                )
+            acc[(t, h)] = results.tile([P, N_TILE], F32, name="acc", bufs=6)
+            nc.vector.tensor_tensor(
+                out=acc[(t, h)][:], in0=lin[:], in1=bias_sb[:, h * N_TILE : (h + 1) * N_TILE], op=ALU.add
+            )
 
         def add_product(engine, t, j, h):
-            cols = slice(h * N_TILE, (h + 1) * N_TILE)
-            engine.tensor_tensor(out=acc[t][:, cols], in0=acc[t][:, cols], in1=product_tiles[(t, j, h)][:], op=ALU.add)
-
-        def products(t, j):
-            for h in range(HALVES):
-                right = next_bank("right")
-                piece = COMPONENTS * t + j
-                multiply(right, xn_codes[:, piece, :], xn_scales[:, piece, :], w_right, w_lr_planes, 4, h, True, True)
-                product_tiles[(t, j, h)] = products_pool.tile([P, N_TILE], F32, name="product")
-                nc.vector.tensor_tensor(
-                    out=product_tiles[(t, j, h)][:], in0=left_copies[(t, j, h)][:], in1=right[:], op=ALU.mult
-                )
-                if (j, h) in GPSIMD_ADDS:
-                    add_product(nc.gpsimd, t, j, h)
+            engine.tensor_tensor(out=acc[(t, h)][:], in0=acc[(t, h)][:], in1=product_tiles[("tile", t, j, h)][:], op=ALU.add)
 
         out_tiles = out.rearrange("(p t) h -> p t h", t=TILES)
 
         def finish(t, h):
-            cols = slice(h * N_TILE, (h + 1) * N_TILE)
-            nc.scalar.activation(out=acc[t][:, cols], in_=acc[t][:, cols], func=ACT.Tanh)
-            nc.sync.dma_start(out=out_tiles[:, t, cols], in_=acc[t][:, cols])
+            nc.scalar.activation(out=acc[(t, h)][:], in_=acc[(t, h)][:], func=ACT.Tanh)
+            nc.sync.dma_start(out=out_tiles[:, t, h * N_TILE : (h + 1) * N_TILE], in_=acc[(t, h)][:])
 
-        lefts(0, 0)
-        linear_half(0, 0)
-        linear_half(0, 1)
-        for step in range(STEPS):
-            t, j = divmod(step, COMPONENTS)
-            later_t, later_j = divmod(step + 1, COMPONENTS)
-            if exists(later_t):
-                lefts(later_t, later_j)
-            if step == 1:
+        unit_terms = {}
+        unit_backs = {}
+
+        def linear_unit(q, u):
+            lin = next_bank("lin")
+            for b in unit_blocks(u):
+                for g in range(INV_PASSES):
+                    pieces = pair_pieces(q, g)
+                    multiply_turned(
+                        lin, b, inv_codes[:, pieces, :], inv_scales[:, pieces, :], w_ii[:, g, :], w_ii_planes, 4 * g,
+                        g == 0, g == INV_PASSES - 1,
+                    )
+            terms = results.tile([P, N_TILE], F32, name="unit_linear", bufs=2)
+            unit_terms[(q, u)] = [terms] + [product_tiles[("unit", q, j, u)] for j in range(COMPONENTS)]
+            for b in unit_blocks(u):
+                cols = slice((b % UNIT_BLOCKS) * PAIR_TOKENS, (b % UNIT_BLOCKS + 1) * PAIR_TOKENS)
+                nc.scalar.activation(out=terms[:, cols], in_=lin[:, cols], func=ACT.Identity, bias=bias_cols[:, b : b + 1])
+
+        def turn_back(q, u):
+            unit_backs[(q, u)] = bank_tile((FIRST_PRODUCT_BANK + len(banks_used)) % BANKS, [P, PAIR, UNIT_BLOCKS, P], "back")
+            banks_used.append("back")
+            for k in range(UNIT_BLOCKS):
+                for s in range(PAIR):
+                    first = (PAIR * k + s) * P
+                    for i, term in enumerate(unit_terms[(q, u)]):
+                        nc.tensor.matmul(
+                            out=unit_backs[(q, u)][:, s, k, :], lhsT=term[:, first : first + P], rhs=identity[:],
+                            is_transpose=True, start=(i == 0), stop=(i == COMPONENTS),
+                        )
+
+        def finish_unit(q, u):
+            width = UNIT_BLOCKS * P
+            result = results.tile([P, PAIR, width], F32, name="result", bufs=2)
+            nc.scalar.activation(out=result[:], in_=unit_backs[(q, u)][:].rearrange("p s k h -> p s (k h)"), func=ACT.Tanh)
+            nc.sync.dma_start(out=out_tiles[:, PAIR * q : PAIR * (q + 1), u * width : (u + 1) * width], in_=result[:])
+
+        jobs = []
+        after = {}
+        before = {}
+
+        def hook(job_index, action):
+            after.setdefault(job_index, []).append(action)
+
+        SEQ = ((((2, 0), (2, 1)), (0, 0)), (((3, 0), (3, 1)), (0, 1)), (((4, 0), (4, 1)), None), (((5, 0), (5, 1)), (0, 2)), (((6, 0), (6, 1)), (0, 3)), (((7, 0), (7, 1)), None))
+        for halves, unit in SEQ:
+            f = len(jobs)
+            index = {}
+            for j in range(COMPONENTS):
+                for k, (t, h) in enumerate(halves):
+                    index[(j, k)] = len(jobs)
+                    jobs.append(("tile", t, j, h))
+                if unit:
+                    q, u = unit
+                    jobs.append(("unit", q, j, u))
+            last = len(jobs) - 1
+            four = unit is not None
+            for k in range(2):
+                t, h = halves[k]
+                if f > 0:
+                    before.setdefault(f - 1, []).append(lambda t=t, h=h: linear_half(t, h))
+            for j, k in GPSIMD_ADDS + (((1, 1),) if four else ()):
+                t, h = halves[k]
+                hook(index[(j, k)], lambda t=t, j=j, h=h: add_product(nc.gpsimd, t, j, h))
+            for j, k in VECTOR_ADDS[1:] if four else VECTOR_ADDS:
+                t, h = halves[k]
+                hook(last, lambda t=t, j=j, h=h: add_product(nc.vector, t, j, h))
+            for k in range(2):
+                t, h = halves[k]
+                hook(last + 2 + k, lambda t=t, h=h: finish(t, h))
+            if unit:
+                hook(last + 2, lambda q=q, u=u: linear_unit(q, u))
+                hook(last + 4, lambda q=q, u=u: turn_back(q, u))
+                hook(last + 5, lambda q=q, u=u: finish_unit(q, u))
+        N = len(jobs)
+        left(jobs[0])
+        left(jobs[1])
+        linear_half(*SEQ[0][0][0])
+        linear_half(*SEQ[0][0][1])
+        for n in range(N + 10):
+            if n + 2 < N:
+                left(jobs[n + 2])
+            if n == 1:
                 nc.scalar.activation(out=warm[:], in_=warm[:], func=ACT.Tanh)
-            products(t, j)
-            if j == COMPONENTS - 1:
-                if exists(t + 1):
-                    linear_half(t + 1, 0)
-                    linear_half(t + 1, 1)
-                for add_j, add_h in VECTOR_ADDS:
-                    add_product(nc.vector, t, add_j, add_h)
-            if j < HALVES and exists(t - 1):
-                finish(t - 1, j)
-        for h in range(HALVES):
-            finish(TILES - 1, h)
+                spread_cols = next_bank("turned_bias")
+                nc.tensor.transpose(spread_cols[:, 0:P], bias_words[:], identity[:])
+                nc.vector.tensor_copy(out=bias_cols[:], in_=spread_cols[:, 0:BLOCKS])
+            if n < N:
+                right(jobs[n])
+            for action in before.get(n, ()):
+                action()
+            for action in after.get(n, ()):
+                action()

@@ -459,7 +459,7 @@ def tile_ryeelman_pa_kernel(
                         g == 0, g == INV_PASSES - 1,
                     )
             terms = results.tile([P, N_TILE], F32, name="unit_linear", bufs=2)
-            unit_terms[(q, u)] = [terms] + [product_tiles[("unit", q, j, u)] for j in range(COMPONENTS)]
+            unit_terms[(q, u)] = [terms] + [product_tiles[("unit", q, j, u)] for j in range(1, COMPONENTS)]
             for b in unit_blocks(u):
                 cols = slice((b % UNIT_BLOCKS) * PAIR_TOKENS, (b % UNIT_BLOCKS + 1) * PAIR_TOKENS)
                 nc.scalar.activation(out=terms[:, cols], in_=lin[:, cols], func=ACT.Identity, bias=bias_cols[:, b : b + 1])
@@ -473,7 +473,7 @@ def tile_ryeelman_pa_kernel(
                     for i, term in enumerate(unit_terms[(q, u)]):
                         nc.tensor.matmul(
                             out=unit_backs[(q, u)][:, s, k, :], lhsT=term[:, first : first + P], rhs=identity[:],
-                            is_transpose=True, start=(i == 0), stop=(i == COMPONENTS),
+                            is_transpose=True, start=(i == 0), stop=(i == COMPONENTS - 1),
                         )
 
         def finish_unit(q, u):
@@ -489,41 +489,56 @@ def tile_ryeelman_pa_kernel(
         def hook(job_index, action):
             after.setdefault(job_index, []).append(action)
 
-        SEQ = ((((2, 0), (2, 1)), (0, 0)), (((3, 0), (3, 1)), (0, 1)), (((4, 0), (4, 1)), None), (((5, 0), (5, 1)), (0, 2)), (((6, 0), (6, 1)), (0, 3)), (((7, 0), (7, 1)), None))
-        for halves, unit in SEQ:
+        TILE_LIST = (((2, 0), (2, 1)), ((3, 0), (3, 1)), ((4, 0), (4, 1)), ((5, 0), (5, 1)), ((6, 0), (6, 1)), ((7, 0), (7, 1)))
+        WOVEN = ((2,4,6),(2,4,6),(),(2,4,6),(2,4,6),())
+        UNIT_LIST = ((0, 0), (0, 1), (0, 2), (0, 3))
+        unit_jobs = [("unit", q, j, u) for q, u in UNIT_LIST for j in range(COMPONENTS)]
+        for e, halves in enumerate(TILE_LIST):
             f = len(jobs)
             index = {}
+            slots = WOVEN[e]
+            n = 0
             for j in range(COMPONENTS):
                 for k, (t, h) in enumerate(halves):
                     index[(j, k)] = len(jobs)
                     jobs.append(("tile", t, j, h))
-                if unit:
-                    q, u = unit
-                    jobs.append(("unit", q, j, u))
+                    n += 1
+                    if n in slots and unit_jobs:
+                        job = unit_jobs.pop(0)
+                        jobs.append(job)
+                        if job[2] == 1:
+                            hook(len(jobs) - 1 + 4, lambda q=job[1], u=job[3]: nc.gpsimd.tensor_tensor(out=product_tiles[("unit", q, 1, u)][:], in0=product_tiles[("unit", q, 0, u)][:], in1=product_tiles[("unit", q, 1, u)][:], op=ALU.add))
+                        if job[2] == COMPONENTS - 1:
+                            q, u = job[1], job[3]
+                            here = len(jobs) - 1
+                            hook(here + 2, lambda q=q, u=u: linear_unit(q, u))
+                            hook(here + 6, lambda q=q, u=u: turn_back(q, u))
+                            hook(here + 7, lambda q=q, u=u: finish_unit(q, u))
             last = len(jobs) - 1
-            four = unit is not None
+            four = e in (0,1,3,4)
             for k in range(2):
                 t, h = halves[k]
                 if f > 0:
                     before.setdefault(f - 1, []).append(lambda t=t, h=h: linear_half(t, h))
-            for j, k in GPSIMD_ADDS + (((1, 1),) if four else ()):
+            final = e == len(TILE_LIST) - 1
+            gadds = GPSIMD_ADDS + (((1, 1),) if four else ())
+            vadds = [(a, last) for a in (VECTOR_ADDS[1:] if four else VECTOR_ADDS)]
+            if final:
+                gadds, vadds = (GPSIMD_ADDS, [(a, last) for a in VECTOR_ADDS])
+            for j, k in gadds:
                 t, h = halves[k]
                 hook(index[(j, k)], lambda t=t, j=j, h=h: add_product(nc.gpsimd, t, j, h))
-            for j, k in VECTOR_ADDS[1:] if four else VECTOR_ADDS:
+            for (j, k), at in vadds:
                 t, h = halves[k]
-                hook(last, lambda t=t, j=j, h=h: add_product(nc.vector, t, j, h))
+                hook(at, lambda t=t, j=j, h=h: add_product(nc.vector, t, j, h))
             for k in range(2):
                 t, h = halves[k]
                 hook(last + 2 + k, lambda t=t, h=h: finish(t, h))
-            if unit:
-                hook(last + 2, lambda q=q, u=u: linear_unit(q, u))
-                hook(last + 4, lambda q=q, u=u: turn_back(q, u))
-                hook(last + 5, lambda q=q, u=u: finish_unit(q, u))
         N = len(jobs)
         left(jobs[0])
         left(jobs[1])
-        linear_half(*SEQ[0][0][0])
-        linear_half(*SEQ[0][0][1])
+        linear_half(*TILE_LIST[0][0])
+        linear_half(*TILE_LIST[0][1])
         for n in range(N + 10):
             if n + 2 < N:
                 left(jobs[n + 2])

@@ -459,10 +459,10 @@ def tile_ryeelman_pa_kernel(
                         g == 0, g == INV_PASSES - 1,
                     )
             terms = results.tile([P, N_TILE], F32, name="unit_linear", bufs=2)
-            unit_terms[(q, u)] = [terms] + [product_tiles[("unit", q, j, u)] for j in range(1, COMPONENTS)]
+            unit_terms[(q, u)] = [terms, product_tiles[("unit", q, 2, u)]]
             for b in unit_blocks(u):
                 cols = slice((b % UNIT_BLOCKS) * PAIR_TOKENS, (b % UNIT_BLOCKS + 1) * PAIR_TOKENS)
-                nc.scalar.activation(out=terms[:, cols], in_=lin[:, cols], func=ACT.Identity, bias=bias_cols[:, b : b + 1])
+                nc.vector.scalar_tensor_tensor(out=terms[:, cols], in0=lin[:, cols], scalar=bias_cols[:, b : b + 1], in1=product_tiles[("unit", q, 1, u)][:, cols], op0=ALU.add, op1=ALU.add)
 
         def turn_back(q, u):
             unit_backs[(q, u)] = bank_tile((FIRST_PRODUCT_BANK + len(banks_used)) % BANKS, [P, PAIR, UNIT_BLOCKS, P], "back")
@@ -473,7 +473,7 @@ def tile_ryeelman_pa_kernel(
                     for i, term in enumerate(unit_terms[(q, u)]):
                         nc.tensor.matmul(
                             out=unit_backs[(q, u)][:, s, k, :], lhsT=term[:, first : first + P], rhs=identity[:],
-                            is_transpose=True, start=(i == 0), stop=(i == COMPONENTS - 1),
+                            is_transpose=True, start=(i == 0), stop=(i == 1),
                         )
 
         def finish_unit(q, u):
@@ -511,7 +511,7 @@ def tile_ryeelman_pa_kernel(
                         if job[2] == COMPONENTS - 1:
                             q, u = job[1], job[3]
                             here = len(jobs) - 1
-                            hook(here + 2, lambda q=q, u=u: linear_unit(q, u))
+                            hook(here + 3, lambda q=q, u=u: linear_unit(q, u))
                             hook(here + 6, lambda q=q, u=u: turn_back(q, u))
                             hook(here + 7, lambda q=q, u=u: finish_unit(q, u))
             last = len(jobs) - 1

@@ -356,7 +356,7 @@ def tile_ryeelman_pa_kernel(
         for h in range(HALVES):
             nc.scalar.copy(out=bias_sb[:, h * N_TILE : (h + 1) * N_TILE], in_=spread[h][:])
         quantise_xn(TURN_BANKS // 2 - 1)
-        for call in range(VECTOR_INV_BANKS // 2, TURN_BANKS // 2):
+        for call in range(VECTOR_INV_BANKS // 2, TURN_BANKS // 2 - 2):
             quantise_inv(call)
 
         banks_used = []
@@ -524,31 +524,35 @@ def tile_ryeelman_pa_kernel(
             gadds = GPSIMD_ADDS + (((1, 1),) if four else ())
             vadds = [(a, last) for a in (VECTOR_ADDS[1:] if four else VECTOR_ADDS)]
             if final:
-                gadds, vadds = (GPSIMD_ADDS, [(a, last) for a in VECTOR_ADDS])
+                gadds, vadds = (((0, 0), (0, 1)), [((1, 0), last), ((1, 1), last), ((2, 0), last), ((2, 1), last)])
             for j, k in gadds:
                 t, h = halves[k]
-                hook(index[(j, k)], lambda t=t, j=j, h=h: add_product(nc.gpsimd, t, j, h))
+                hook(max(index[(j, k)], 0), lambda t=t, j=j, h=h: add_product(nc.gpsimd, t, j, h))
             for (j, k), at in vadds:
                 t, h = halves[k]
                 hook(at, lambda t=t, j=j, h=h: add_product(nc.vector, t, j, h))
             for k in range(2):
                 t, h = halves[k]
-                hook(last + 2 + k, lambda t=t, h=h: finish(t, h))
+                hook(last + (4, 6)[k], lambda t=t, h=h: finish(t, h))
         N = len(jobs)
+        hook(5, lambda: quantise_inv(4))
+        hook(14, lambda: quantise_inv(5))
         left(jobs[0])
         left(jobs[1])
-        linear_half(*TILE_LIST[0][0])
-        linear_half(*TILE_LIST[0][1])
         for n in range(N + 10):
             if n + 2 < N:
                 left(jobs[n + 2])
-            if n == 1:
+            if n == 7:
                 nc.scalar.activation(out=warm[:], in_=warm[:], func=ACT.Tanh)
+            if n == 1:
                 spread_cols = next_bank("turned_bias")
                 nc.tensor.transpose(spread_cols[:, 0:P], bias_words[:], identity[:])
                 nc.vector.tensor_copy(out=bias_cols[:], in_=spread_cols[:, 0:BLOCKS])
             if n < N:
                 right(jobs[n])
+            if n == 0:
+                linear_half(*TILE_LIST[0][0])
+                linear_half(*TILE_LIST[0][1])
             for action in before.get(n, ()):
                 action()
             for action in after.get(n, ()):

@@ -39,15 +39,17 @@ PAIR_TILES = 2
 BANK_PIECES = 2
 CALL_PIECES = 4
 TURN_BANKS = PIECES // BANK_PIECES
-VECTOR_INV_BANKS = 6
+VECTOR_INV_BANKS = 4
 HEAD_INV_BANKS = 3
-PREP_BUFS = 3
+PREP_BUFS = 4
 SQUARE_BUFS = 2
 COPY_BUFS = 8
 PRODUCT_BUFS = 8
 GPSIMD_ADDS = ((0, 0), (0, 1), (1, 0))
 VECTOR_ADDS = ((1, 1), (2, 0), (2, 1))
 BLOCKS = HIDDEN // P
+SU = (3,)
+QU = ()
 UNIT_BLOCKS = 2
 PAIR_TOKENS = PAIR * P
 
@@ -142,17 +144,18 @@ def tile_ryeelman_pa_kernel(
         nc.sync.dma_start(out=first_channel[:], in_=equivariant_input.rearrange("(p t) j -> p (t j)", t=TILES))
         load_first_hidden(0)
         load_eq(0)
-        load_first_hidden(1)
         for t in range(PAIR_TILES):
             nc.sync.dma_start(out=inv_sb[:, t, 0:INPUT_FEATURES], in_=input_features[:, t, :])
         for t in range(PAIR_TILES):
             nc.sync.dma_start(out=inv_sb[:, t, INPUT_FEATURES:FEATURES], in_=hidden_features[:, t, :])
         load_eq(1)
-        for q in range(2, TILES // PAIR):
-            load_first_hidden(q)
-        for t in range(2, TILES // 2):
-            load_eq(t)
-            load_inv(t)
+        load_first_hidden(1)
+        load_eq(2)
+        load_inv(2)
+        load_eq(3)
+        load_first_hidden(2)
+        load_inv(3)
+        load_first_hidden(3)
         nc.sync.dma_start(out=bias_row[0:1, :], in_=b_ii.rearrange("(o h) -> o h", o=1))
         nc.sync.dma_start(out=bias_rows[0:BLOCKS, :], in_=b_ii.rearrange("(r h) -> r h", r=BLOCKS))
         for t in range(TILES // 2, TILES):
@@ -238,6 +241,8 @@ def tile_ryeelman_pa_kernel(
                 func=ACT.Abs_reciprocal_sqrt,
                 bias=EPSILON,
             )
+
+        def square_root(t):
             nc.scalar.activation(out=recip[:, t, :], in_=recip[:, t, :], func=ACT.Square)
 
         def turn_eq(b):
@@ -301,7 +306,6 @@ def tile_ryeelman_pa_kernel(
             return 0 <= t < TILES
 
         place_first_hidden(0)
-        place_first_hidden(1)
         square(0)
         turn_inv(0)
         copy_inv(0)
@@ -311,24 +315,27 @@ def tile_ryeelman_pa_kernel(
         square(1)
         turn_eq(0)
         turn_inv(2)
-        for q in range(2, TILES // PAIR):
-            place_first_hidden(q)
         quantise_inv(0)
         reciprocal(0)
+        square_root(0)
         copy_inv(2)
+        place_first_hidden(1)
         add_squares(1)
         square(2)
         scale_xn(0)
         for b in range(HEAD_INV_BANKS, VECTOR_INV_BANKS):
             turn_inv(b)
             copy_inv(b)
-            if b == HEAD_INV_BANKS + 1:
+            if b == HEAD_INV_BANKS:
                 quantise_inv(1)
+        place_first_hidden(2)
         eq_done = 1
         for t in range(1, TILES):
+            if t == 2:
+                place_first_hidden(3)
             if exists(t + 1):
                 add_squares(t + 1)
-            if exists(t + 2):
+            if exists(t + 2) and t < 1:
                 square(t + 2)
             eq_until = (COMPONENTS * (t + 1)) // BANK_PIECES
             for b in range(eq_done, eq_until):
@@ -336,12 +343,13 @@ def tile_ryeelman_pa_kernel(
             if TILES - 1 - len(INV_BANKS) <= t < TILES - 1:
                 turn_inv(VECTOR_INV_BANKS + t - (TILES - 1 - len(INV_BANKS)))
             reciprocal(t)
+            if exists(t + 2) and t >= 1:
+                square(t + 2)
+            square_root(t)
             for b in range(eq_done, eq_until):
                 scale_xn(b)
                 if b % 2 == 0:
                     quantise_xn(b // 2 - 1)
-            if t == 1:
-                quantise_inv(2)
             eq_done = eq_until
         spread = [bank_tile(SUM_BANKS[h], [P, N_TILE], "spread%d" % h) for h in range(HALVES)]
         for h in range(HALVES):
@@ -356,7 +364,7 @@ def tile_ryeelman_pa_kernel(
         for h in range(HALVES):
             nc.scalar.copy(out=bias_sb[:, h * N_TILE : (h + 1) * N_TILE], in_=spread[h][:])
         quantise_xn(TURN_BANKS // 2 - 1)
-        for call in range(VECTOR_INV_BANKS // 2, TURN_BANKS // 2 - 2):
+        for call in range(VECTOR_INV_BANKS // 2, TURN_BANKS // 2):
             quantise_inv(call)
 
         banks_used = []
@@ -459,10 +467,13 @@ def tile_ryeelman_pa_kernel(
                         g == 0, g == INV_PASSES - 1,
                     )
             terms = results.tile([P, N_TILE], F32, name="unit_linear", bufs=2)
-            unit_terms[(q, u)] = [terms, product_tiles[("unit", q, 2, u)]]
+            unit_terms[(q, u)] = [terms] + ([product_tiles[("unit", q, 1, u)]] if u in SU else []) + ([] if u in QU else [product_tiles[("unit", q, 2, u)]])
             for b in unit_blocks(u):
                 cols = slice((b % UNIT_BLOCKS) * PAIR_TOKENS, (b % UNIT_BLOCKS + 1) * PAIR_TOKENS)
-                nc.vector.scalar_tensor_tensor(out=terms[:, cols], in0=lin[:, cols], scalar=bias_cols[:, b : b + 1], in1=product_tiles[("unit", q, 1, u)][:, cols], op0=ALU.add, op1=ALU.add)
+                if u in SU:
+                    nc.scalar.activation(out=terms[:, cols], in_=lin[:, cols], func=ACT.Identity, bias=bias_cols[:, b : b + 1])
+                else:
+                    nc.vector.scalar_tensor_tensor(out=terms[:, cols], in0=lin[:, cols], scalar=bias_cols[:, b : b + 1], in1=product_tiles[("unit", q, 1, u)][:, cols], op0=ALU.add, op1=ALU.add)
 
         def turn_back(q, u):
             unit_backs[(q, u)] = bank_tile((FIRST_PRODUCT_BANK + len(banks_used)) % BANKS, [P, PAIR, UNIT_BLOCKS, P], "back")
@@ -473,7 +484,7 @@ def tile_ryeelman_pa_kernel(
                     for i, term in enumerate(unit_terms[(q, u)]):
                         nc.tensor.matmul(
                             out=unit_backs[(q, u)][:, s, k, :], lhsT=term[:, first : first + P], rhs=identity[:],
-                            is_transpose=True, start=(i == 0), stop=(i == 1),
+                            is_transpose=True, start=(i == 0), stop=(i == len(unit_terms[(q, u)]) - 1),
                         )
 
         def finish_unit(q, u):
@@ -508,6 +519,8 @@ def tile_ryeelman_pa_kernel(
                         jobs.append(job)
                         if job[2] == 1:
                             hook(len(jobs) - 1 + 4, lambda q=job[1], u=job[3]: nc.gpsimd.tensor_tensor(out=product_tiles[("unit", q, 1, u)][:], in0=product_tiles[("unit", q, 0, u)][:], in1=product_tiles[("unit", q, 1, u)][:], op=ALU.add))
+                            if job[3] in QU:
+                                hook(len(jobs) - 1 + 4, lambda q=job[1], u=job[3]: nc.gpsimd.tensor_tensor(out=product_tiles[("unit", q, 1, u)][:], in0=product_tiles[("unit", q, 2, u)][:], in1=product_tiles[("unit", q, 1, u)][:], op=ALU.add))
                         if job[2] == COMPONENTS - 1:
                             q, u = job[1], job[3]
                             here = len(jobs) - 1
@@ -533,10 +546,8 @@ def tile_ryeelman_pa_kernel(
                 hook(at, lambda t=t, j=j, h=h: add_product(nc.vector, t, j, h))
             for k in range(2):
                 t, h = halves[k]
-                hook(last + (4, 6)[k], lambda t=t, h=h: finish(t, h))
+                hook(last + (2, 3)[k], lambda t=t, h=h: finish(t, h))
         N = len(jobs)
-        hook(5, lambda: quantise_inv(4))
-        hook(14, lambda: quantise_inv(5))
         left(jobs[0])
         left(jobs[1])
         for n in range(N + 10):

@@ -48,6 +48,7 @@ PRODUCT_BUFS = 8
 GPSIMD_ADDS = ((0, 0), (0, 1), (1, 0))
 VECTOR_ADDS = ((1, 1), (2, 0), (2, 1))
 BLOCKS = HIDDEN // P
+PB = (1, 3)
 SU = (3,)
 QU = ()
 UNIT_BLOCKS = 2
@@ -89,7 +90,8 @@ def tile_ryeelman_pa_kernel(
         first_channel = keep.tile([P, TILES * COMPONENTS], BF16)
         first_hidden = keep.tile([P, TILES * COMPONENTS, FILL], BF16)
         eq_sb = keep.tile([P, TILES * COMPONENTS, CHANNELS], BF16)
-        inv_sb = keep.tile([P, TILES, FEATURES], BF16)
+        input_sb = keep.tile([P, TILES, INPUT_FEATURES], BF16)
+        hidden_sb = keep.tile([P, TILES, HIDDEN], BF16)
         bias_row = keep.tile([P, HIDDEN], BF16)
         ones = keep.tile([P, P], BF16)
         bias_sb = keep.tile([P, HIDDEN], BF16)
@@ -134,9 +136,10 @@ def tile_ryeelman_pa_kernel(
             rows = slice(COMPONENTS * t, COMPONENTS * (t + 1))
             nc.sync.dma_start(out=eq_sb[:, rows, FILL:CHANNELS], in_=hidden_vectors[:, rows, FILL - 1 :])
 
-        def load_inv(t):
-            nc.sync.dma_start(out=inv_sb[:, t, 0:INPUT_FEATURES], in_=input_features[:, t, :])
-            nc.sync.dma_start(out=inv_sb[:, t, INPUT_FEATURES:FEATURES], in_=hidden_features[:, t, :])
+        def load_inv(first, count):
+            tiles = slice(first, first + count)
+            nc.sync.dma_start(out=input_sb[:, tiles, :], in_=input_features[:, tiles, :])
+            nc.sync.dma_start(out=hidden_sb[:, tiles, :], in_=hidden_features[:, tiles, :])
 
         def load_words(dst, words):
             nc.sync.dma_start(out=dst.bitcast(I32), in_=words.rearrange("p n t -> p (n t)").bitcast(I32))
@@ -144,34 +147,24 @@ def tile_ryeelman_pa_kernel(
         nc.sync.dma_start(out=first_channel[:], in_=equivariant_input.rearrange("(p t) j -> p (t j)", t=TILES))
         load_first_hidden(0)
         load_eq(0)
-        for t in range(PAIR_TILES):
-            nc.sync.dma_start(out=inv_sb[:, t, 0:INPUT_FEATURES], in_=input_features[:, t, :])
-        for t in range(PAIR_TILES):
-            nc.sync.dma_start(out=inv_sb[:, t, INPUT_FEATURES:FEATURES], in_=hidden_features[:, t, :])
+        nc.sync.dma_start(out=bias_row[0:1, :], in_=b_ii.rearrange("(o h) -> o h", o=1))
+        load_inv(0, PAIR_TILES)
         load_eq(1)
         load_first_hidden(1)
         load_eq(2)
-        load_inv(2)
+        load_inv(2, 1)
         load_eq(3)
         load_first_hidden(2)
-        load_inv(3)
+        load_eq(4)
+        load_eq(5)
         load_first_hidden(3)
-        nc.sync.dma_start(out=bias_row[0:1, :], in_=b_ii.rearrange("(o h) -> o h", o=1))
+        load_eq(6)
+        load_inv(3, 1)
+        load_eq(7)
         nc.sync.dma_start(out=bias_rows[0:BLOCKS, :], in_=b_ii.rearrange("(r h) -> r h", r=BLOCKS))
-        for t in range(TILES // 2, TILES):
-            load_eq(t)
-        for t in range(TILES // 2, TILES):
-            load_inv(t)
+        load_inv(4, 2)
         load_words(w_left[:], W_left_words[0])
         load_words(w_right[:], W_right_words[0])
-        for g in range(INV_PASSES):
-            load_words(w_ii[:, g, :], W_ii_words[g])
-        for quadrant in range(4):
-            rows = slice(4 * quadrant, 4 * quadrant + 4)
-            nc.sync.dma_start(
-                out=w_ii_planes[32 * quadrant : 32 * quadrant + 4 * INV_PASSES, :].bitcast(I32),
-                in_=W_ii_scales[:, rows, :].bitcast(I32),
-            )
         for quadrant in range(4):
             rows = slice(4 * quadrant, 4 * quadrant + 4)
             nc.sync.dma_start(
@@ -181,6 +174,15 @@ def tile_ryeelman_pa_kernel(
             nc.sync.dma_start(
                 out=w_lr_planes[32 * quadrant + 4 : 32 * quadrant + 8, :].bitcast(I32),
                 in_=W_right_scales[0, rows, :].bitcast(I32),
+            )
+        load_inv(6, 2)
+        for g in range(INV_PASSES):
+            load_words(w_ii[:, g, :], W_ii_words[g])
+        for quadrant in range(4):
+            rows = slice(4 * quadrant, 4 * quadrant + 4)
+            nc.sync.dma_start(
+                out=w_ii_planes[32 * quadrant : 32 * quadrant + 4 * INV_PASSES, :].bitcast(I32),
+                in_=W_ii_scales[:, rows, :].bitcast(I32),
             )
 
         nc.vector.tensor_copy(out=eq_sb[:, :, 0:1], in_=first_channel[:].unsqueeze(2))
@@ -254,7 +256,8 @@ def tile_ryeelman_pa_kernel(
             turned_inv[b] = bank_tile(INV_BANKS[b % len(INV_BANKS)], [P, BANK_PIECES, 2, P], "turned_inv")
             for s in range(BANK_PIECES):
                 t, g = part_of(BANK_PIECES * b + s)
-                transpose_words(turned_inv[b], s, inv_sb[:, t, g * K_PASS : (g + 1) * K_PASS].bitcast(F32))
+                source = input_sb[:, t, :] if g == 0 else hidden_sb[:, t, (g - 1) * K_PASS : g * K_PASS]
+                transpose_words(turned_inv[b], s, source.bitcast(F32))
 
         def scale_xn(b):
             for s in range(BANK_PIECES):
@@ -307,6 +310,12 @@ def tile_ryeelman_pa_kernel(
 
         place_first_hidden(0)
         square(0)
+        for h in range(HALVES):
+            spread = bank_tile(EQ_BANKS[1 + h], [P, N_TILE], "spread")
+            nc.tensor.matmul(
+                out=spread[:], lhsT=ones[:], rhs=bias_row[:, h * N_TILE : (h + 1) * N_TILE], start=True, stop=True
+            )
+            nc.scalar.copy(out=bias_sb[:, h * N_TILE : (h + 1) * N_TILE], in_=spread[:])
         turn_inv(0)
         copy_inv(0)
         turn_inv(1)
@@ -316,10 +325,10 @@ def tile_ryeelman_pa_kernel(
         turn_eq(0)
         turn_inv(2)
         quantise_inv(0)
+        place_first_hidden(1)
         reciprocal(0)
         square_root(0)
         copy_inv(2)
-        place_first_hidden(1)
         add_squares(1)
         square(2)
         scale_xn(0)
@@ -351,18 +360,11 @@ def tile_ryeelman_pa_kernel(
                 if b % 2 == 0:
                     quantise_xn(b // 2 - 1)
             eq_done = eq_until
-        spread = [bank_tile(SUM_BANKS[h], [P, N_TILE], "spread%d" % h) for h in range(HALVES)]
-        for h in range(HALVES):
-            nc.tensor.matmul(
-                out=spread[h][:], lhsT=ones[:], rhs=bias_row[:, h * N_TILE : (h + 1) * N_TILE], start=True, stop=True
-            )
         for b in range(VECTOR_INV_BANKS, TURN_BANKS):
             if b >= VECTOR_INV_BANKS + len(INV_BANKS):
                 turn_inv(b)
             copy_inv(b)
         nc.vector.tensor_copy(out=bias_words[:], in_=bias_rows[:])
-        for h in range(HALVES):
-            nc.scalar.copy(out=bias_sb[:, h * N_TILE : (h + 1) * N_TILE], in_=spread[h][:])
         quantise_xn(TURN_BANKS // 2 - 1)
         for call in range(VECTOR_INV_BANKS // 2, TURN_BANKS // 2):
             quantise_inv(call)
@@ -427,7 +429,7 @@ def tile_ryeelman_pa_kernel(
 
         def right(job):
             bank = factor(job, w_right, w_lr_planes, 4, "right")
-            product_tiles[job] = products_pool.tile([P, N_TILE], F32, name=job[0] + "_product", bufs=8 if job[0] == "tile" else 6)
+            product_tiles[job] = products_pool.tile([P, N_TILE], F32, name=job[0] + "_product", bufs=8 if job[0] == "tile" else 8)
             nc.vector.tensor_tensor(out=product_tiles[job][:], in0=left_copies[job][:], in1=bank[:], op=ALU.mult)
 
         acc = {}
@@ -466,7 +468,7 @@ def tile_ryeelman_pa_kernel(
                         lin, b, inv_codes[:, pieces, :], inv_scales[:, pieces, :], w_ii[:, g, :], w_ii_planes, 4 * g,
                         g == 0, g == INV_PASSES - 1,
                     )
-            terms = results.tile([P, N_TILE], F32, name="unit_linear", bufs=2)
+            terms = results.tile([P, N_TILE], F32, name="unit_linear", bufs=3)
             unit_terms[(q, u)] = [terms] + ([product_tiles[("unit", q, 1, u)]] if u in SU else []) + ([] if u in QU else [product_tiles[("unit", q, 2, u)]])
             for b in unit_blocks(u):
                 cols = slice((b % UNIT_BLOCKS) * PAIR_TOKENS, (b % UNIT_BLOCKS + 1) * PAIR_TOKENS)
@@ -525,14 +527,18 @@ def tile_ryeelman_pa_kernel(
                             q, u = job[1], job[3]
                             here = len(jobs) - 1
                             hook(here + 3, lambda q=q, u=u: linear_unit(q, u))
-                            hook(here + 6, lambda q=q, u=u: turn_back(q, u))
-                            hook(here + 7, lambda q=q, u=u: finish_unit(q, u))
+                            if u in PB:
+                                hook(here + 6, lambda q=q, u=u: turn_back(q, u - 1))
+                                hook(here + 7, lambda q=q, u=u: finish_unit(q, u - 1))
+                            if u + 1 not in PB:
+                                hook(here + 6, lambda q=q, u=u: turn_back(q, u))
+                                hook(here + 7 + (1 if u in PB else 0), lambda q=q, u=u: finish_unit(q, u))
             last = len(jobs) - 1
             four = e in (0,1,3,4)
             for k in range(2):
                 t, h = halves[k]
                 if f > 0:
-                    before.setdefault(f - 1, []).append(lambda t=t, h=h: linear_half(t, h))
+                    before.setdefault(f - (4, 2)[k], []).append(lambda t=t, h=h: linear_half(t, h))
             final = e == len(TILE_LIST) - 1
             gadds = GPSIMD_ADDS + (((1, 1),) if four else ())
             vadds = [(a, last) for a in (VECTOR_ADDS[1:] if four else VECTOR_ADDS)]

from contextlib import ExitStack

import concourse.mybir as mybir
from concourse.masks import make_identity

F32 = mybir.dt.float32
BF16 = mybir.dt.bfloat16
I32 = mybir.dt.int32
U32 = mybir.dt.uint32
U8 = mybir.dt.uint8
FP8X4 = mybir.dt.float8_e4m3fn_x4
ALU = mybir.AluOpType
ACT = mybir.ActivationFunctionType

P = 128
TOKENS = 1024
TILES = TOKENS // P
COMPONENTS = 3
CHANNELS = 512
INPUT_FEATURES = 512
FEATURES = 1536
HIDDEN = 1024
K_PASS = 512
PACK = 4
INV_PASSES = FEATURES // K_PASS
WORDS = K_PASS // 2
N_TILE = 512
HALVES = HIDDEN // N_TILE
EPSILON = 1e-6
FILL = 16
PAIR = 2
BANKS = 8
SUM_BANKS = (0, 1)
EQ_BANKS = (2, 3, 4)
INV_BANKS = (5, 6, 7)
FIRST_PRODUCT_BANK = 2
PIECES = COMPONENTS * TILES
PAIR_TILES = 2
BANK_PIECES = 2
CALL_PIECES = 4
TURN_BANKS = PIECES // BANK_PIECES
VECTOR_INV_BANKS = 4
HEAD_INV_BANKS = 3
PREP_BUFS = 4
SQUARE_BUFS = 2
COPY_BUFS = 8
PRODUCT_BUFS = 8
GPSIMD_ADDS = ((0, 0), (0, 1), (1, 0))
VECTOR_ADDS = ((1, 1), (2, 0), (2, 1))
BLOCKS = HIDDEN // P
PB = (1, 3)
SU = (3,)
QU = ()
UNIT_BLOCKS = 2
PAIR_TOKENS = PAIR * P

FLOPS = 2 * TOKENS * HIDDEN * (2 * COMPONENTS * CHANNELS + FEATURES)


def tile_ryeelman_pa_kernel(
    tc,
    invariant_input,
    equivariant_input,
    invariant_hidden,
    equivariant_hidden,
    W_left_words,
    W_left_scales,
    W_right_words,
    W_right_scales,
    W_ii_words,
    W_ii_scales,
    b_ii,
    out,
):
    nc = tc.nc
    with ExitStack() as ctx:
        ctx.enter_context(tc.manual_schedule())
        keep = ctx.enter_context(tc.tile_pool(name="keep", bufs=1))
        prep = ctx.enter_context(tc.tile_pool(name="prep", bufs=PREP_BUFS))
        square_pool = ctx.enter_context(tc.tile_pool(name="square_pool", bufs=SQUARE_BUFS))
        copies = ctx.enter_context(tc.tile_pool(name="copies", bufs=COPY_BUFS))
        products_pool = ctx.enter_context(tc.tile_pool(name="products", bufs=PRODUCT_BUFS))
        results = ctx.enter_context(tc.tile_pool(name="results", bufs=6))
        psum = ctx.enter_context(tc.psum_pool(name="psum", bufs=1))

        def bank_tile(b, shape, name):
            return psum.tile(shape, F32, tag="bank%d" % b, name=name)

        identity = keep.tile([P, P], F32)
        first_channel = keep.tile([P, TILES * COMPONENTS], BF16)
        first_hidden = keep.tile([P, TILES * COMPONENTS, FILL], BF16)
        eq_sb = keep.tile([P, TILES * COMPONENTS, CHANNELS], BF16)
        input_sb = keep.tile([P, TILES, INPUT_FEATURES], BF16)
        hidden_sb = keep.tile([P, TILES, HIDDEN], BF16)
        bias_row = keep.tile([P, HIDDEN], BF16)
        ones = keep.tile([P, P], BF16)
        bias_sb = keep.tile([P, HIDDEN], BF16)
        w_ii = keep.tile([P, INV_PASSES, HIDDEN], U32, align_bytes=64)
        w_left = keep.tile([P, HIDDEN], U32, align_bytes=64)
        w_right = keep.tile([P, HIDDEN], U32, align_bytes=64)
        w_ii_planes = keep.tile([P, HIDDEN], U8, align_bytes=64)
        w_lr_planes = keep.tile([P, HIDDEN], U8, align_bytes=64)
        xn_codes = keep.tile([P, PIECES, P], U32, align_bytes=64)
        xn_scales = keep.tile([P, PIECES, P], U8, align_bytes=64)
        inv_codes = keep.tile([P, PIECES, P], U32, align_bytes=64)
        inv_scales = keep.tile([P, PIECES, P], U8, align_bytes=64)
        recip = keep.tile([P, TILES, CHANNELS], F32)
        acc = {}
        bias_rows = keep.tile([P, P], BF16)
        bias_words = keep.tile([P, P], F32)
        bias_cols = keep.tile([P, BLOCKS], F32)

        make_identity(nc, identity[:])
        warm = keep.tile([P, 1], F32)
        nc.vector.memset(warm[:], 1.0)
        nc.scalar.activation(out=warm[:], in_=warm[:], func=ACT.Abs_reciprocal_sqrt)
        nc.vector.memset(w_ii_planes[:].bitcast(I32), 0)
        nc.vector.memset(w_lr_planes[:].bitcast(I32), 0)
        nc.vector.memset(bias_row[:].bitcast(I32), 0)
        nc.vector.memset(bias_rows[:].bitcast(I32), 0)
        nc.vector.memset(ones[:], 1.0)

        hidden_vectors = equivariant_hidden.rearrange("(p t) j c -> p (t j) c", t=TILES)
        input_features = invariant_input.rearrange("(p t) k -> p t k", t=TILES)
        hidden_features = invariant_hidden.rearrange("(p t) k -> p t k", t=TILES)

        def load_first_hidden(q):
            rows = slice(PAIR * COMPONENTS * q, PAIR * COMPONENTS * (q + 1))
            nc.sync.dma_start(out=first_hidden[:, rows, 0 : FILL - 1], in_=hidden_vectors[:, rows, 0 : FILL - 1])

        def place_first_hidden(q):
            rows = slice(PAIR * COMPONENTS * q, PAIR * COMPONENTS * (q + 1))
            nc.vector.tensor_copy(out=eq_sb[:, rows, 1:FILL], in_=first_hidden[:, rows, 0 : FILL - 1])

        def load_eq(t):
            rows = slice(COMPONENTS * t, COMPONENTS * (t + 1))
            nc.sync.dma_start(out=eq_sb[:, rows, FILL:CHANNELS], in_=hidden_vectors[:, rows, FILL - 1 :])

        def load_inv(first, count):
            tiles = slice(first, first + count)
            nc.sync.dma_start(out=input_sb[:, tiles, :], in_=input_features[:, tiles, :])
            nc.sync.dma_start(out=hidden_sb[:, tiles, :], in_=hidden_features[:, tiles, :])

        def load_words(dst, words):
            nc.sync.dma_start(out=dst.bitcast(I32), in_=words.rearrange("p n t -> p (n t)").bitcast(I32))

        nc.sync.dma_start(out=first_channel[:], in_=equivariant_input.rearrange("(p t) j -> p (t j)", t=TILES))
        load_first_hidden(0)
        load_eq(0)
        nc.sync.dma_start(out=bias_row[0:1, :], in_=b_ii.rearrange("(o h) -> o h", o=1))
        load_inv(0, PAIR_TILES)
        load_eq(1)
        load_first_hidden(1)
        load_eq(2)
        load_inv(2, 1)
        load_eq(3)
        load_first_hidden(2)
        load_eq(4)
        load_eq(5)
        load_first_hidden(3)
        load_eq(6)
        load_inv(3, 1)
        load_eq(7)
        nc.sync.dma_start(out=bias_rows[0:BLOCKS, :], in_=b_ii.rearrange("(r h) -> r h", r=BLOCKS))
        load_inv(4, 2)
        load_words(w_left[:], W_left_words[0])
        load_words(w_right[:], W_right_words[0])
        for quadrant in range(4):
            rows = slice(4 * quadrant, 4 * quadrant + 4)
            nc.sync.dma_start(
                out=w_lr_planes[32 * quadrant : 32 * quadrant + 4, :].bitcast(I32),
                in_=W_left_scales[0, rows, :].bitcast(I32),
            )
            nc.sync.dma_start(
                out=w_lr_planes[32 * quadrant + 4 : 32 * quadrant + 8, :].bitcast(I32),
                in_=W_right_scales[0, rows, :].bitcast(I32),
            )
        load_inv(6, 2)
        for g in range(INV_PASSES):
            load_words(w_ii[:, g, :], W_ii_words[g])
        for quadrant in range(4):
            rows = slice(4 * quadrant, 4 * quadrant + 4)
            nc.sync.dma_start(
                out=w_ii_planes[32 * quadrant : 32 * quadrant + 4 * INV_PASSES, :].bitcast(I32),
                in_=W_ii_scales[:, rows, :].bitcast(I32),
            )

        nc.vector.tensor_copy(out=eq_sb[:, :, 0:1], in_=first_channel[:].unsqueeze(2))

        def transpose_words(bank, slot, words):
            for u in range(2):
                nc.tensor.transpose(bank[:, slot, u, :], words[:, u:WORDS:2], identity[:])

        def piece_of(t, j):
            if t < PAIR_TILES:
                return PAIR * COMPONENTS * (t // PAIR) + PAIR * j + t % PAIR
            return COMPONENTS * t + j

        def part_of(piece):
            if piece < COMPONENTS * PAIR_TILES:
                q, rest = divmod(piece, PAIR * COMPONENTS)
                return PAIR * q + rest % PAIR, rest // PAIR
            return divmod(piece, COMPONENTS)

        squares = {}
        sums = {}
        turned_eq = {}
        turned_inv = {}
        grouped_xn = {}
        grouped_inv = {}

        def square(t):
            squares[t] = square_pool.tile([P, COMPONENTS, CHANNELS], F32, name="squares")
            scalars = COMPONENTS - 1
            nc.scalar.activation(
                out=squares[t][:, 0:scalars, :].rearrange("p j (r c) -> p j r c", r=PACK),
                in_=eq_sb[:, COMPONENTS * t : COMPONENTS * t + scalars, :].rearrange("p j (c r) -> p j r c", r=PACK),
                func=ACT.Square,
            )
            third = eq_sb[:, COMPONENTS * t + scalars, :].rearrange("p (c r) -> p r c", r=PACK)
            for r in range(PACK):
                nc.gpsimd.tensor_tensor(
                    out=squares[t][:, scalars, r * P : (r + 1) * P], in0=third[:, r, :], in1=third[:, r, :], op=ALU.mult
                )

        def add_squares(t):
            sums[t] = bank_tile(SUM_BANKS[t % len(SUM_BANKS)], [P, PACK, P], "sums")
            for r in range(PACK):
                for j in range(COMPONENTS):
                    nc.tensor.matmul(
                        out=sums[t][:, r, :],
                        lhsT=squares[t][:, j, r * P : (r + 1) * P],
                        rhs=identity[:],
                        is_transpose=True,
                        start=(j == 0),
                        stop=(j == COMPONENTS - 1),
                    )

        def reciprocal(t):
            nc.scalar.activation(
                out=recip[:, t, :].rearrange("p (c r) -> p c r", r=PACK),
                in_=sums[t][:].rearrange("p r c -> p c r"),
                func=ACT.Abs_reciprocal_sqrt,
                bias=EPSILON,
            )

        def square_root(t):
            nc.scalar.activation(out=recip[:, t, :], in_=recip[:, t, :], func=ACT.Square)

        def turn_eq(b):
            turned_eq[b] = bank_tile(EQ_BANKS[b % len(EQ_BANKS)], [P, BANK_PIECES, 2, P], "turned_eq")
            for s in range(BANK_PIECES):
                transpose_words(turned_eq[b], s, eq_sb[:, BANK_PIECES * b + s, :].bitcast(F32))

        def turn_inv(b):
            turned_inv[b] = bank_tile(INV_BANKS[b % len(INV_BANKS)], [P, BANK_PIECES, 2, P], "turned_inv")
            for s in range(BANK_PIECES):
                t, g = part_of(BANK_PIECES * b + s)
                source = input_sb[:, t, :] if g == 0 else hidden_sb[:, t, (g - 1) * K_PASS : g * K_PASS]
                transpose_words(turned_inv[b], s, source.bitcast(F32))

        def scale_xn(b):
            for s in range(BANK_PIECES):
                t, j = divmod(BANK_PIECES * b + s, COMPONENTS)
                call, place = divmod(piece_of(t, j), CALL_PIECES)
                if call not in grouped_xn:
                    grouped_xn[call] = prep.tile([P, CALL_PIECES, P, 2, 2], BF16, name="grouped_xn", align_bytes=64)
                nc.vector.tensor_tensor(
                    out=grouped_xn[call][:, place, :, :, :],
                    in0=turned_eq[b][:, s, :, :]
                    .rearrange("p u c -> p (u c)")
                    .bitcast(BF16)
                    .rearrange("p (u c e) -> p c u e", u=2, e=2),
                    in1=recip[:, t, :].rearrange("p (c u e) -> p c u e", u=2, e=2),
                    op=ALU.mult,
                )

        def copy_inv(b):
            call, half = divmod(b, CALL_PIECES // BANK_PIECES)
            if half == 0:
                grouped_inv[call] = prep.tile([P, CALL_PIECES, P, PACK], BF16, name="grouped_inv", align_bytes=64)
            dst = (
                grouped_inv[call][:, BANK_PIECES * half : BANK_PIECES * (half + 1), :, :]
                .rearrange("p s c k -> p (s c k)")
                .bitcast(F32)
                .rearrange("p (s c u) -> p s c u", s=BANK_PIECES, u=2)
            )
            src = turned_inv[b][:].rearrange("p s u c -> p s c u")
            if b < VECTOR_INV_BANKS:
                nc.vector.tensor_copy(out=dst, in_=src)
            else:
                nc.scalar.copy(out=dst, in_=src)

        def quantise(codes, scales, grouped, call):
            pieces = slice(CALL_PIECES * call, CALL_PIECES * (call + 1))
            nc.vector.quantize_mx(
                out=codes[:, pieces, :].rearrange("p s c -> p (s c)").bitcast(FP8X4),
                scales=scales[:, pieces, :].rearrange("p s c -> p (s c)"),
                in_=grouped,
            )

        def quantise_xn(call):
            quantise(xn_codes, xn_scales, grouped_xn[call][:].rearrange("p s c u e -> p (s c u e)"), call)

        def quantise_inv(call):
            quantise(inv_codes, inv_scales, grouped_inv[call][:].rearrange("p s c k -> p (s c k)"), call)

        def exists(t):
            return 0 <= t < TILES

        place_first_hidden(0)
        square(0)
        for h in range(HALVES):
            spread = bank_tile(EQ_BANKS[1 + h], [P, N_TILE], "spread")
            nc.tensor.matmul(
                out=spread[:], lhsT=ones[:], rhs=bias_row[:, h * N_TILE : (h + 1) * N_TILE], start=True, stop=True
            )
            nc.scalar.copy(out=bias_sb[:, h * N_TILE : (h + 1) * N_TILE], in_=spread[:])
        turn_inv(0)
        copy_inv(0)
        turn_inv(1)
        copy_inv(1)
        add_squares(0)
        square(1)
        turn_eq(0)
        turn_inv(2)
        quantise_inv(0)
        place_first_hidden(1)
        reciprocal(0)
        square_root(0)
        copy_inv(2)
        add_squares(1)
        square(2)
        scale_xn(0)
        for b in range(HEAD_INV_BANKS, VECTOR_INV_BANKS):
            turn_inv(b)
            copy_inv(b)
            if b == HEAD_INV_BANKS:
                quantise_inv(1)
        place_first_hidden(2)
        eq_done = 1
        for t in range(1, TILES):
            if t == 2:
                place_first_hidden(3)
            if exists(t + 1):
                add_squares(t + 1)
            if exists(t + 2) and t < 1:
                square(t + 2)
            eq_until = (COMPONENTS * (t + 1)) // BANK_PIECES
            for b in range(eq_done, eq_until):
                turn_eq(b)
            if TILES - 1 - len(INV_BANKS) <= t < TILES - 1:
                turn_inv(VECTOR_INV_BANKS + t - (TILES - 1 - len(INV_BANKS)))
            reciprocal(t)
            if exists(t + 2) and t >= 1:
                square(t + 2)
            square_root(t)
            for b in range(eq_done, eq_until):
                scale_xn(b)
                if b % 2 == 0:
                    quantise_xn(b // 2 - 1)
            eq_done = eq_until
        for b in range(VECTOR_INV_BANKS, TURN_BANKS):
            if b >= VECTOR_INV_BANKS + len(INV_BANKS):
                turn_inv(b)
            copy_inv(b)
        nc.vector.tensor_copy(out=bias_words[:], in_=bias_rows[:])
        quantise_xn(TURN_BANKS // 2 - 1)
        for call in range(VECTOR_INV_BANKS // 2, TURN_BANKS // 2):
            quantise_inv(call)

        banks_used = []

        def next_bank(name):
            banks_used.append(name)
            return bank_tile((FIRST_PRODUCT_BANK + len(banks_used) - 1) % BANKS, [P, N_TILE], name)

        def multiply(bank, codes, scales, words, planes, first_row, h, start, stop):
            cols = slice(h * N_TILE, (h + 1) * N_TILE)
            nc.tensor.matmul_mx(
                out=bank[:],
                lhsT=codes.bitcast(FP8X4),
                lhsT_scale=scales,
                rhs=words[:, cols].bitcast(FP8X4),
                rhs_scale=planes[first_row:P, cols],
                start=start,
                stop=stop,
            )

        def multiply_turned(bank, b, codes, scales, words, planes, first_row, start, stop):
            cols = slice((b % UNIT_BLOCKS) * PAIR_TOKENS, (b % UNIT_BLOCKS + 1) * PAIR_TOKENS)
            hidden = slice(b * P, (b + 1) * P)
            nc.tensor.matmul_mx(
                out=bank[:, cols],
                lhsT=words[:, hidden].bitcast(FP8X4),
                lhsT_scale=planes[first_row:P, hidden],
                rhs=codes.rearrange("p s c -> p (s c)").bitcast(FP8X4),
                rhs_scale=scales.rearrange("p s c -> p (s c)"),
                start=start,
                stop=stop,
            )

        def pair_pieces(q, j):
            first = PAIR * COMPONENTS * q + PAIR * j
            return slice(first, first + PAIR)

        def unit_blocks(u):
            return range(UNIT_BLOCKS * u, UNIT_BLOCKS * (u + 1))

        def factor(job, words, planes, first_row, name):
            kind, i, j, h = job
            bank = next_bank(name)
            if kind == "tile":
                piece = piece_of(i, j)
                multiply(bank, xn_codes[:, piece, :], xn_scales[:, piece, :], words, planes, first_row, h, True, True)
            else:
                pieces = pair_pieces(i, j)
                for b in unit_blocks(h):
                    multiply_turned(bank, b, xn_codes[:, pieces, :], xn_scales[:, pieces, :], words, planes, first_row, True, True)
            return bank

        left_copies = {}
        product_tiles = {}

        def left(job):
            bank = factor(job, w_left, w_lr_planes, 0, "left")
            left_copies[job] = copies.tile([P, N_TILE], F32, name="left_sb")
            nc.scalar.copy(out=left_copies[job][:], in_=bank[:])

        def right(job):
            bank = factor(job, w_right, w_lr_planes, 4, "right")
            product_tiles[job] = products_pool.tile([P, N_TILE], F32, name=job[0] + "_product", bufs=8 if job[0] == "tile" else 8)
            nc.vector.tensor_tensor(out=product_tiles[job][:], in0=left_copies[job][:], in1=bank[:], op=ALU.mult)

        acc = {}

        def linear_half(t, h):
            lin = next_bank("lin")
            for g in range(INV_PASSES):
                piece = piece_of(t, g)
                multiply(
                    lin, inv_codes[:, piece, :], inv_scales[:, piece, :], w_ii[:, g, :], w_ii_planes, 4 * g, h,
                    g == 0, g == INV_PASSES - 1,
                )
            acc[(t, h)] = results.tile([P, N_TILE], F32, name="acc", bufs=6)
            nc.vector.tensor_tensor(
                out=acc[(t, h)][:], in0=lin[:], in1=bias_sb[:, h * N_TILE : (h + 1) * N_TILE], op=ALU.add
            )

        def add_product(engine, t, j, h):
            engine.tensor_tensor(out=acc[(t, h)][:], in0=acc[(t, h)][:], in1=product_tiles[("tile", t, j, h)][:], op=ALU.add)

        out_tiles = out.rearrange("(p t) h -> p t h", t=TILES)

        def finish(t, h):
            nc.scalar.activation(out=acc[(t, h)][:], in_=acc[(t, h)][:], func=ACT.Tanh)
            nc.sync.dma_start(out=out_tiles[:, t, h * N_TILE : (h + 1) * N_TILE], in_=acc[(t, h)][:])

        unit_terms = {}
        unit_backs = {}

        def linear_unit(q, u):
            lin = next_bank("lin")
            for b in unit_blocks(u):
                for g in range(INV_PASSES):
                    pieces = pair_pieces(q, g)
                    multiply_turned(
                        lin, b, inv_codes[:, pieces, :], inv_scales[:, pieces, :], w_ii[:, g, :], w_ii_planes, 4 * g,
                        g == 0, g == INV_PASSES - 1,
                    )
            terms = results.tile([P, N_TILE], F32, name="unit_linear", bufs=3)
            unit_terms[(q, u)] = [terms] + ([product_tiles[("unit", q, 1, u)]] if u in SU else []) + ([] if u in QU else [product_tiles[("unit", q, 2, u)]])
            for b in unit_blocks(u):
                cols = slice((b % UNIT_BLOCKS) * PAIR_TOKENS, (b % UNIT_BLOCKS + 1) * PAIR_TOKENS)
                if u in SU:
                    nc.scalar.activation(out=terms[:, cols], in_=lin[:, cols], func=ACT.Identity, bias=bias_cols[:, b : b + 1])
                else:
                    nc.vector.scalar_tensor_tensor(out=terms[:, cols], in0=lin[:, cols], scalar=bias_cols[:, b : b + 1], in1=product_tiles[("unit", q, 1, u)][:, cols], op0=ALU.add, op1=ALU.add)

        def turn_back(q, u):
            unit_backs[(q, u)] = bank_tile((FIRST_PRODUCT_BANK + len(banks_used)) % BANKS, [P, PAIR, UNIT_BLOCKS, P], "back")
            banks_used.append("back")
            for k in range(UNIT_BLOCKS):
                for s in range(PAIR):
                    first = (PAIR * k + s) * P
                    for i, term in enumerate(unit_terms[(q, u)]):
                        nc.tensor.matmul(
                            out=unit_backs[(q, u)][:, s, k, :], lhsT=term[:, first : first + P], rhs=identity[:],
                            is_transpose=True, start=(i == 0), stop=(i == len(unit_terms[(q, u)]) - 1),
                        )

        def finish_unit(q, u):
            width = UNIT_BLOCKS * P
            result = results.tile([P, PAIR, width], F32, name="result", bufs=2)
            nc.scalar.activation(out=result[:], in_=unit_backs[(q, u)][:].rearrange("p s k h -> p s (k h)"), func=ACT.Tanh)
            nc.sync.dma_start(out=out_tiles[:, PAIR * q : PAIR * (q + 1), u * width : (u + 1) * width], in_=result[:])

        jobs = []
        after = {}
        before = {}

        def hook(job_index, action):
            after.setdefault(job_index, []).append(action)

        TILE_LIST = (((2, 0), (2, 1)), ((3, 0), (3, 1)), ((4, 0), (4, 1)), ((5, 0), (5, 1)), ((6, 0), (6, 1)), ((7, 0), (7, 1)))
        WOVEN = ((2,4,6),(2,4,6),(),(2,4,6),(2,4,6),())
        UNIT_LIST = ((0, 0), (0, 1), (0, 2), (0, 3))
        unit_jobs = [("unit", q, j, u) for q, u in UNIT_LIST for j in range(COMPONENTS)]
        for e, halves in enumerate(TILE_LIST):
            f = len(jobs)
            index = {}
            slots = WOVEN[e]
            n = 0
            for j in range(COMPONENTS):
                for k, (t, h) in enumerate(halves):
                    index[(j, k)] = len(jobs)
                    jobs.append(("tile", t, j, h))
                    n += 1
                    if n in slots and unit_jobs:
                        job = unit_jobs.pop(0)
                        jobs.append(job)
                        if job[2] == 1:
                            hook(len(jobs) - 1 + 4, lambda q=job[1], u=job[3]: nc.gpsimd.tensor_tensor(out=product_tiles[("unit", q, 1, u)][:], in0=product_tiles[("unit", q, 0, u)][:], in1=product_tiles[("unit", q, 1, u)][:], op=ALU.add))
                            if job[3] in QU:
                                hook(len(jobs) - 1 + 4, lambda q=job[1], u=job[3]: nc.gpsimd.tensor_tensor(out=product_tiles[("unit", q, 1, u)][:], in0=product_tiles[("unit", q, 2, u)][:], in1=product_tiles[("unit", q, 1, u)][:], op=ALU.add))
                        if job[2] == COMPONENTS - 1:
                            q, u = job[1], job[3]
                            here = len(jobs) - 1
                            hook(here + 3, lambda q=q, u=u: linear_unit(q, u))
                            if u in PB:
                                hook(here + 6, lambda q=q, u=u: turn_back(q, u - 1))
                                hook(here + 7, lambda q=q, u=u: finish_unit(q, u - 1))
                            if u + 1 not in PB:
                                hook(here + 6, lambda q=q, u=u: turn_back(q, u))
                                hook(here + 7 + (1 if u in PB else 0), lambda q=q, u=u: finish_unit(q, u))
            last = len(jobs) - 1
            four = e in (0,1,3,4)
            for k in range(2):
                t, h = halves[k]
                if f > 0:
                    before.setdefault(f - (4, 2)[k], []).append(lambda t=t, h=h: linear_half(t, h))
            final = e == len(TILE_LIST) - 1
            gadds = GPSIMD_ADDS + (((1, 1),) if four else ())
            vadds = [(a, last) for a in (VECTOR_ADDS[1:] if four else VECTOR_ADDS)]
            if final:
                gadds, vadds = (((0, 0), (0, 1)), [((1, 0), last), ((1, 1), last), ((2, 0), last), ((2, 1), last)])
            for j, k in gadds:
                t, h = halves[k]
                hook(max(index[(j, k)], 0), lambda t=t, j=j, h=h: add_product(nc.gpsimd, t, j, h))
            for (j, k), at in vadds:
                t, h = halves[k]
                hook(at, lambda t=t, j=j, h=h: add_product(nc.vector, t, j, h))
            for k in range(2):
                t, h = halves[k]
                hook(last + (2, 3)[k], lambda t=t, h=h: finish(t, h))
        N = len(jobs)
        left(jobs[0])
        left(jobs[1])
        for n in range(N + 10):
            if n + 2 < N:
                left(jobs[n + 2])
            if n == 7:
                nc.scalar.activation(out=warm[:], in_=warm[:], func=ACT.Tanh)
            if n == 1:
                spread_cols = next_bank("turned_bias")
                nc.tensor.transpose(spread_cols[:, 0:P], bias_words[:], identity[:])
                nc.vector.tensor_copy(out=bias_cols[:], in_=spread_cols[:, 0:BLOCKS])
            if n < N:
                right(jobs[n])
            if n == 0:
                linear_half(*TILE_LIST[0][0])
                linear_half(*TILE_LIST[0][1])
            for action in before.get(n, ()):
                action()
            for action in after.get(n, ()):
                action()
